import numpy as np
import ml_dtypes


def mxq(x, axis, fmt="e4m3"):
    dtype, down = {"e4m3": (ml_dtypes.float8_e4m3fn, 7), "e5m2": (ml_dtypes.float8_e5m2, 14)}[fmt]
    v = np.moveaxis(np.asarray(x, np.float32).astype(ml_dtypes.bfloat16).astype(np.float64), axis, -1)
    blocks = v.reshape(v.shape[:-1] + (-1, 32))
    amax = np.abs(blocks).max(-1, keepdims=True)
    byte = np.maximum(np.where(amax > 0, np.frexp(amax)[1] - 1 + 127, 0) - down, 1)
    scale = np.exp2(byte - 127.0)
    codes = (blocks / scale).astype(np.float32).astype(dtype).astype(np.float64)
    return np.moveaxis((codes * scale).reshape(v.shape), -1, axis)


WIDE = False


def mx_kscale(k):
    if not WIDE:
        return np.ones(k)
    levels = np.array([10, -10, 5, -5, 0])
    a = np.random.permutation(np.resize(levels, k // 512 * 4)).reshape(k // 512, 4)
    idx = np.arange(k)
    return np.exp2(a[idx // 512, idx % 128 // 32])


BF16 = ml_dtypes.bfloat16


def bf(x):
    return np.asarray(x, np.float32).astype(BF16)


def f64(x):
    return np.asarray(x).astype(np.float64)


B, D, H = 256, 512, 2048
C = D + H


def sigmoid(v):
    return 1.0 / (1.0 + np.exp(-v))


def silu(v):
    return v / (1.0 + np.exp(-v))


def setup_inputs():
    s = mx_kscale(C)
    return {"x": bf(np.random.standard_normal((B, D)) * s[:D]),
            "hidden_state": bf(np.random.standard_normal((B, H)) * s[D:]),
            "W_r": bf(np.random.standard_normal((C, H)) / np.sqrt(C) / s[:, None]),
            "b_r": bf(np.random.standard_normal(H) * 0.3),
            "W_g": bf(np.random.standard_normal((C, H)) * 1.5 / np.sqrt(C) / s[:, None]),
            "b_g": bf(np.random.standard_normal(H) * 0.3),
            "W_up": bf(np.random.standard_normal((C, H)) * 1.5 / np.sqrt(C) / s[:, None]),
            "b_up": bf(np.random.standard_normal(H) * 0.3)}


def reference(x, hidden_state, W_r, b_r, W_g, b_g, W_up, b_up):
    h = f64(hidden_state)
    W_r, W_g, W_up = f64(W_r), f64(W_g), f64(W_up)
    xq = mxq(f64(x), 1, "e4m3")
    hq = mxq(h, 1, "e4m3")
    r = sigmoid((xq @ mxq(W_r[:D], 0, "e4m3")) + (hq @ mxq(W_r[D:], 0, "e4m3")) + f64(b_r))
    rhq = mxq(r * h, 1, "e4m3")
    gate = (xq @ mxq(W_g[:D], 0, "e4m3")) + (rhq @ mxq(W_g[D:], 0, "e4m3")) + f64(b_g)
    up = (xq @ mxq(W_up[:D], 0, "e4m3")) + (rhq @ mxq(W_up[D:], 0, "e4m3")) + f64(b_up)
    return silu(gate) * up

@@ -1,0 +1,209 @@
+from contextlib import ExitStack
+
+import concourse.mybir as mybir
+from concourse.masks import make_identity
+
+FP8X4 = mybir.dt.float8_e4m3fn_x4
+BF16 = mybir.dt.bfloat16
+F32 = mybir.dt.float32
+U32 = mybir.dt.uint32
+U8 = mybir.dt.uint8
+ACT = mybir.ActivationFunctionType
+ALU = mybir.AluOpType
+
+P = 128
+PACK = 4
+K_PASS = P * PACK
+
+B, D, H = 256, 512, 2048
+C = D + H
+CHUNKS = C // K_PASS
+BLOCK = PACK * P
+BLOCKS = H // BLOCK
+H_TILES = H // P
+B_TILES = B // P
+RUN = 4
+RAW_BUFS = 3
+
+FLOPS = 2 * B * C * H * 3
+
+
+def tile_recurrentffn_pa_kernel(tc, x, hidden_state, W_r, b_r, W_g, b_g, W_up, b_up, out):
+    nc = tc.nc
+    weights = [W_r, W_g, W_up]
+    with ExitStack() as ctx:
+        const = ctx.enter_context(tc.tile_pool(name="const", bufs=1))
+        staging = ctx.enter_context(tc.tile_pool(name="staging", bufs=RAW_BUFS))
+        regroup = ctx.enter_context(tc.tile_pool(name="regroup", bufs=4))
+        quantised = ctx.enter_context(tc.tile_pool(name="quantised", bufs=2))
+        work = ctx.enter_context(tc.tile_pool(name="work", bufs=2))
+        stores = ctx.enter_context(tc.tile_pool(name="stores", bufs=4))
+        psum_acc = ctx.enter_context(tc.psum_pool(name="psum_acc", bufs=4))
+        psum_tr = ctx.enter_context(tc.psum_pool(name="psum_tr", bufs=4))
+
+        raw_tiles = {}
+
+        def load_next_chunk():
+            q = len(raw_tiles)
+            if q == len(weights) * CHUNKS:
+                return
+            g = q % CHUNKS
+            rows = weights[q // CHUNKS][g * K_PASS : (g + 1) * K_PASS, :].rearrange("(t p) n -> p t n", p=P)
+            raw = staging.tile([P, PACK, H], BF16, tag="raw")
+            width = BLOCK if q == 0 else H
+            for n0 in range(0, H, width):
+                nc.sync.dma_start(out=raw[:, :, n0 : n0 + width], in_=rows[:, :, n0 : n0 + width])
+            raw_tiles[q] = raw
+
+        load_next_chunk()
+
+        acts_sb = staging.tile([P, B_TILES, C], BF16, tag="raw")
+        nc.sync.dma_start(out=acts_sb[:, :, 0:D], in_=x.rearrange("(s p) d -> p s d", p=P))
+        nc.sync.dma_start(out=acts_sb[:, :, D:C], in_=hidden_state.rearrange("(s p) d -> p s d", p=P))
+        load_next_chunk()
+
+        bias_rows = const.tile([P, P], BF16)
+        nc.vector.memset(bias_rows[:], 0.0)
+        for w, b in enumerate([b_r, b_g, b_up]):
+            nc.scalar.dma_start(
+                out=bias_rows[w * H_TILES : (w + 1) * H_TILES, :],
+                in_=b.rearrange("(i p) -> i p", p=P),
+            )
+
+        ident_bf = const.tile([P, P], BF16)
+        make_identity(nc, ident_bf[:])
+        ident_f32 = const.tile([P, P], F32)
+        make_identity(nc, ident_f32[:])
+
+        bias = const.tile([P, P], F32)
+        acts_grouped = const.tile([P, CHUNKS, B, PACK], BF16, align_bytes=64)
+        acts_codes = const.tile([P, CHUNKS, B], U32, align_bytes=64)
+        acts_scales = const.tile([P, CHUNKS, B], U8, align_bytes=64)
+        rh_codes = const.tile([P, BLOCKS, B], U32, align_bytes=64)
+        rh_scales = const.tile([P, BLOCKS, B], U8, align_bytes=64)
+        silu_gate = const.tile([P, H_TILES, B], F32)
+
+        def prepare_activations():
+            bias_ps = psum_tr.tile([P, P], BF16, tag="tr")
+            nc.tensor.transpose(bias_ps[:], bias_rows[:], ident_bf[:])
+            nc.vector.tensor_copy(out=bias[:], in_=bias_ps[:])
+            for g in range(CHUNKS):
+                acts_ps = psum_tr.tile([P, PACK, B], BF16, tag="tr")
+                for t in range(PACK):
+                    k0 = g * K_PASS + t * P
+                    for s in range(B_TILES):
+                        nc.tensor.transpose(acts_ps[:, t, s * P : (s + 1) * P], acts_sb[:, s, k0 : k0 + P], ident_bf[:])
+                if g % 2 == 0:
+                    nc.scalar.copy(out=acts_grouped[:, g, :, :], in_=acts_ps[:].rearrange("p t b -> p b t"))
+                else:
+                    nc.vector.tensor_copy(out=acts_grouped[:, g, :, :], in_=acts_ps[:].rearrange("p t b -> p b t"))
+            for g in range(CHUNKS):
+                nc.vector.quantize_mx(
+                    out=acts_codes[:, g, :].bitcast(FP8X4),
+                    scales=acts_scales[:, g, :],
+                    in_=acts_grouped[:, g, :, :].rearrange("p b t -> p (b t)"),
+                )
+
+        x_and_h = [(acts_codes[:, g, :], acts_scales[:, g, :]) for g in range(CHUNKS)]
+        x_and_rh = x_and_h[0:1] + [(rh_codes[:, c, :], rh_scales[:, c, :]) for c in range(BLOCKS)]
+
+        def finish_reset(c, accs):
+            r_sb = work.tile([P, PACK, B], F32, tag="four_tiles")
+            for t in range(PACK):
+                i = c * PACK + t
+                nc.scalar.activation(out=r_sb[:, t, :], in_=accs[t][:], func=ACT.Sigmoid, bias=bias[:, i : i + 1])
+            rh_grouped = work.tile([P, B, PACK], BF16, align_bytes=64)
+            nc.vector.tensor_tensor(
+                out=rh_grouped[:],
+                in0=r_sb[:].rearrange("p t b -> p b t"),
+                in1=acts_grouped[:, c + 1, :, :],
+                op=ALU.mult,
+            )
+            nc.vector.quantize_mx(
+                out=rh_codes[:, c, :].bitcast(FP8X4),
+                scales=rh_scales[:, c, :],
+                in_=rh_grouped[:].rearrange("p b t -> p (b t)"),
+            )
+
+        def finish_gate(c, accs):
+            for t in range(PACK):
+                i = c * PACK + t
+                nc.scalar.activation(
+                    out=silu_gate[:, i, :], in_=accs[t][:], func=ACT.Silu, bias=bias[:, H_TILES + i : H_TILES + i + 1]
+                )
+
+        def finish_up(c, accs):
+            product = work.tile([P, PACK, B], F32, tag="four_tiles")
+            for t in range(PACK):
+                i = c * PACK + t
+                nc.vector.scalar_tensor_tensor(
+                    out=product[:, t, :],
+                    in0=accs[t][:],
+                    scalar=bias[:, 2 * H_TILES + i : 2 * H_TILES + i + 1],
+                    in1=silu_gate[:, i, :],
+                    op0=ALU.add,
+                    op1=ALU.mult,
+                )
+            for s in range(B_TILES):
+                out_ps = psum_tr.tile([P, BLOCK], F32, tag="tr")
+                for t in range(PACK):
+                    nc.tensor.transpose(out_ps[:, t * P : (t + 1) * P], product[:, t, s * P : (s + 1) * P], ident_f32[:])
+                out_sb = stores.tile([P, BLOCK], F32)
+                if s % 2 == 0:
+                    nc.scalar.copy(out=out_sb[:], in_=out_ps[:])
+                else:
+                    nc.vector.tensor_copy(out=out_sb[:], in_=out_ps[:])
+                nc.sync.dma_start(out=out[s * P : (s + 1) * P, c * BLOCK : (c + 1) * BLOCK], in_=out_sb[:])
+
+        def stream_weight(w, moving, finish_block):
+            codes = quantised.tile([P, CHUNKS, H], U32, align_bytes=64, tag="w_codes")
+            scales = quantised.tile([P, CHUNKS, H], U8, align_bytes=64, tag="w_scales")
+
+            def quantise_piece(g, c):
+                cols = slice(c * BLOCK, (c + 1) * BLOCK)
+                grouped = regroup.tile([P, BLOCK, PACK], BF16, align_bytes=64)
+                source = raw_tiles[w * CHUNKS + g][:, :, cols].rearrange("p t (n i) -> p n t i", i=RUN)
+                target = grouped[:].rearrange("p (n i) t -> p n t i", i=RUN)
+                if (g + c) % 2 == 0:
+                    nc.vector.tensor_copy(out=target, in_=source)
+                else:
+                    nc.scalar.copy(out=target, in_=source)
+                nc.vector.quantize_mx(
+                    out=codes[:, g, cols].bitcast(FP8X4),
+                    scales=scales[:, g, cols],
+                    in_=grouped[:].rearrange("p n t -> p (n t)"),
+                )
+
+            def passes(c, accs, chunks):
+                for g in chunks:
+                    for t in range(PACK):
+                        cols = slice(c * BLOCK + t * P, c * BLOCK + (t + 1) * P)
+                        nc.tensor.matmul_mx(
+                            out=accs[t][:],
+                            lhsT=codes[:, g, cols].bitcast(FP8X4),
+                            lhsT_scale=scales[:, g, cols],
+                            rhs=moving[g][0].bitcast(FP8X4),
+                            rhs_scale=moving[g][1],
+                            start=(g == 0),
+                            stop=(g == CHUNKS - 1),
+                        )
+
+            last = CHUNKS - 1
+            for g in range(last):
+                for c in range(BLOCKS):
+                    quantise_piece(g, c)
+                load_next_chunk()
+                if w == 0 and g == 0:
+                    prepare_activations()
+                    load_next_chunk()
+            for c in range(BLOCKS):
+                accs = [psum_acc.tile([P, B], F32, name="acc", tag="acc") for t in range(PACK)]
+                passes(c, accs, range(last))
+                quantise_piece(last, c)
+                passes(c, accs, [last])
+                finish_block(c, accs)
+            load_next_chunk()
+
+        stream_weight(0, x_and_h, finish_reset)
+        stream_weight(1, x_and_rh, finish_gate)
+        stream_weight(2, x_and_rh, finish_up)

@@ -23,7 +23,11 @@ BLOCKS = H // BLOCK
 H_TILES = H // P
 B_TILES = B // P
 RUN = 4
-RAW_BUFS = 3
+WEIGHTS = 3
+WHOLE = CHUNKS - 2
+STEPS = CHUNKS * BLOCKS // 2
+TOTAL_STEPS = WEIGHTS * STEPS
+BANKS = 8
 
 FLOPS = 2 * B * C * H * 3
 
@@ -33,49 +37,72 @@ def tile_recurrentffn_pa_kernel(tc, x, hidden_state, W_r, b_r, W_g, b_g, W_up, b
     weights = [W_r, W_g, W_up]
     with ExitStack() as ctx:
         const = ctx.enter_context(tc.tile_pool(name="const", bufs=1))
-        staging = ctx.enter_context(tc.tile_pool(name="staging", bufs=RAW_BUFS))
+        staging_whole = ctx.enter_context(tc.tile_pool(name="staging_whole", bufs=WHOLE))
+        staging_pair = ctx.enter_context(tc.tile_pool(name="staging_pair", bufs=1))
         regroup = ctx.enter_context(tc.tile_pool(name="regroup", bufs=4))
-        quantised = ctx.enter_context(tc.tile_pool(name="quantised", bufs=2))
+        quantised = ctx.enter_context(tc.tile_pool(name="quantised", bufs=CHUNKS + 1))
         work = ctx.enter_context(tc.tile_pool(name="work", bufs=2))
         stores = ctx.enter_context(tc.tile_pool(name="stores", bufs=4))
-        psum_acc = ctx.enter_context(tc.psum_pool(name="psum_acc", bufs=4))
-        psum_tr = ctx.enter_context(tc.psum_pool(name="psum_tr", bufs=4))
+        psum = ctx.enter_context(tc.psum_pool(name="psum", bufs=1))
+        ctx.enter_context(tc.manual_schedule())
 
-        raw_tiles = {}
+        whole_tiles = {}
+        pair_tiles = {}
 
-        def load_next_chunk():
-            q = len(raw_tiles)
-            if q == len(weights) * CHUNKS:
+        def rows_of(w, g):
+            return weights[w][g * K_PASS : (g + 1) * K_PASS, :].rearrange("(p t) n -> p t n", t=PACK)
+
+        def load_whole(w, g):
+            if w >= WEIGHTS:
                 return
-            g = q % CHUNKS
-            rows = weights[q // CHUNKS][g * K_PASS : (g + 1) * K_PASS, :].rearrange("(t p) n -> p t n", p=P)
-            raw = staging.tile([P, PACK, H], BF16, tag="raw")
-            width = BLOCK if q == 0 else H
+            raw = staging_whole.tile([P, PACK, H], BF16, tag="whole")
+            width = 2 * BLOCK if w == 0 else H
             for n0 in range(0, H, width):
-                nc.sync.dma_start(out=raw[:, :, n0 : n0 + width], in_=rows[:, :, n0 : n0 + width])
-            raw_tiles[q] = raw
+                nc.sync.dma_start(out=raw[:, :, n0 : n0 + width], in_=rows_of(w, g)[:, :, n0 : n0 + width])
+            whole_tiles[(w, g)] = raw
 
-        load_next_chunk()
+        def load_pair(w):
+            if w >= WEIGHTS:
+                return
+            raw = staging_pair.tile([P, 2, PACK, H], BF16, tag="pair")
+            width = BLOCK if w == 0 else H
+            for n0 in range(0, H, width):
+                for j in range(2):
+                    nc.sync.dma_start(
+                        out=raw[:, j, :, n0 : n0 + width], in_=rows_of(w, WHOLE + j)[:, :, n0 : n0 + width]
+                    )
+            pair_tiles[w] = raw
 
-        acts_sb = staging.tile([P, B_TILES, C], BF16, tag="raw")
-        nc.sync.dma_start(out=acts_sb[:, :, 0:D], in_=x.rearrange("(s p) d -> p s d", p=P))
-        nc.sync.dma_start(out=acts_sb[:, :, D:C], in_=hidden_state.rearrange("(s p) d -> p s d", p=P))
-        load_next_chunk()
-
+        b_r_sb = const.tile([P, BLOCKS, PACK], BF16)
+        nc.scalar.dma_start(out=b_r_sb[:], in_=b_r.rearrange("(c p t) -> p c t", p=P, t=PACK))
         bias_rows = const.tile([P, P], BF16)
         nc.vector.memset(bias_rows[:], 0.0)
-        for w, b in enumerate([b_r, b_g, b_up]):
+        for w, b in [(1, b_g), (2, b_up)]:
             nc.scalar.dma_start(
                 out=bias_rows[w * H_TILES : (w + 1) * H_TILES, :],
                 in_=b.rearrange("(i p) -> i p", p=P),
             )
+
+        load_whole(0, 0)
+        acts_sb = const.tile([P, B_TILES, C], BF16)
+        nc.sync.dma_start(out=acts_sb[:, :, 0:D], in_=x.rearrange("(s p) d -> p s d", p=P))
+        nc.sync.dma_start(out=acts_sb[:, :, D:C], in_=hidden_state.rearrange("(s p) d -> p s d", p=P))
+        for g in range(1, WHOLE):
+            load_whole(0, g)
+        load_pair(0)
 
         ident_bf = const.tile([P, P], BF16)
         make_identity(nc, ident_bf[:])
         ident_f32 = const.tile([P, P], F32)
         make_identity(nc, ident_f32[:])
 
+        zero = const.tile([P, 1], F32)
+        nc.vector.memset(zero[:], 0.0)
+        half = const.tile([P, 1], F32)
+        nc.scalar.activation(out=half[:], in_=zero[:], func=ACT.Sigmoid)
+
         bias = const.tile([P, P], F32)
+
         acts_grouped = const.tile([P, CHUNKS, B, PACK], BF16, align_bytes=64)
         acts_codes = const.tile([P, CHUNKS, B], U32, align_bytes=64)
         acts_scales = const.tile([P, CHUNKS, B], U8, align_bytes=64)
@@ -83,127 +110,209 @@ def tile_recurrentffn_pa_kernel(tc, x, hidden_state, W_r, b_r, W_g, b_g, W_up, b
         rh_scales = const.tile([P, BLOCKS, B], U8, align_bytes=64)
         silu_gate = const.tile([P, H_TILES, B], F32)
 
-        def prepare_activations():
-            bias_ps = psum_tr.tile([P, P], BF16, tag="tr")
-            nc.tensor.transpose(bias_ps[:], bias_rows[:], ident_bf[:])
-            nc.vector.tensor_copy(out=bias[:], in_=bias_ps[:])
+        acts_ps = {}
+
+        def transpose_activations():
             for g in range(CHUNKS):
-                acts_ps = psum_tr.tile([P, PACK, B], BF16, tag="tr")
-                for t in range(PACK):
-                    k0 = g * K_PASS + t * P
+                acts_ps[g] = psum.tile([P, 2, B], F32, name="acts_ps", tag="bank%d" % g)
+                for u in range(2):
                     for s in range(B_TILES):
-                        nc.tensor.transpose(acts_ps[:, t, s * P : (s + 1) * P], acts_sb[:, s, k0 : k0 + P], ident_bf[:])
-                if g % 2 == 0:
-                    nc.scalar.copy(out=acts_grouped[:, g, :, :], in_=acts_ps[:].rearrange("p t b -> p b t"))
-                else:
-                    nc.vector.tensor_copy(out=acts_grouped[:, g, :, :], in_=acts_ps[:].rearrange("p t b -> p b t"))
-            for g in range(CHUNKS):
-                nc.vector.quantize_mx(
-                    out=acts_codes[:, g, :].bitcast(FP8X4),
-                    scales=acts_scales[:, g, :],
-                    in_=acts_grouped[:, g, :, :].rearrange("p b t -> p (b t)"),
-                )
+                        words = acts_sb[:, s, g * K_PASS : (g + 1) * K_PASS].bitcast(F32)
+                        nc.tensor.transpose(
+                            acts_ps[g][:, u, s * P : (s + 1) * P],
+                            words.rearrange("p (j u) -> p j u", u=2)[:, :, u],
+                            ident_f32[:],
+                        )
+            acts_ps[CHUNKS] = psum.tile([P, P], BF16, name="bias_ps", tag="bank%d" % CHUNKS)
+            nc.tensor.transpose(acts_ps[CHUNKS][:], bias_rows[:], ident_bf[:])
+
+        def copy_activations(g):
+            nc.scalar.copy(
+                out=acts_grouped[:, g, :, :].rearrange("p b t -> p (b t)").bitcast(F32).rearrange("p (b u) -> p b u", u=2),
+                in_=acts_ps[g][:].rearrange("p u b -> p b u"),
+            )
+
+        def quantise_activations(g):
+            nc.vector.quantize_mx(
+                out=acts_codes[:, g, :].bitcast(FP8X4),
+                scales=acts_scales[:, g, :],
+                in_=acts_grouped[:, g, :, :].rearrange("p b t -> p (b t)"),
+            )
 
         x_and_h = [(acts_codes[:, g, :], acts_scales[:, g, :]) for g in range(CHUNKS)]
         x_and_rh = x_and_h[0:1] + [(rh_codes[:, c, :], rh_scales[:, c, :]) for c in range(BLOCKS)]
+        moving = [x_and_h, x_and_rh, x_and_rh]
 
-        def finish_reset(c, accs):
-            r_sb = work.tile([P, PACK, B], F32, tag="four_tiles")
-            for t in range(PACK):
-                i = c * PACK + t
-                nc.scalar.activation(out=r_sb[:, t, :], in_=accs[t][:], func=ACT.Sigmoid, bias=bias[:, i : i + 1])
-            rh_grouped = work.tile([P, B, PACK], BF16, align_bytes=64)
-            nc.vector.tensor_tensor(
-                out=rh_grouped[:],
-                in0=r_sb[:].rearrange("p t b -> p b t"),
-                in1=acts_grouped[:, c + 1, :, :],
-                op=ALU.mult,
+        grouped_of = {}
+        codes_of = {}
+
+        def regroup_columns(copy, w, g, c, n0, n1):
+            if n0 == 0:
+                grouped_of[(w, g, c)] = regroup.tile([P, BLOCK, PACK], BF16, name="grouped", align_bytes=64)
+            raw = whole_tiles[(w, g)] if g < WHOLE else pair_tiles[w][:, g - WHOLE]
+            assert w > 0 or (n0, n1) == (0, BLOCK)
+            places = "p (i n) t -> p n t i" if w == 0 else "p (n i) t -> p n t i"
+            copy(
+                out=grouped_of[(w, g, c)][:, n0:n1, :].rearrange(places, i=RUN),
+                in_=raw[:, :, c * BLOCK + n0 : c * BLOCK + n1].rearrange("p t (n i) -> p n t i", i=RUN),
             )
+
+        def quantise_piece(w, g, c):
+            if c == 0:
+                codes = quantised.tile([P, H], U32, align_bytes=64, tag="w_codes")
+                scales = quantised.tile([P, H], U8, align_bytes=64, tag="w_scales")
+                codes_of[(w, g)] = (codes, scales)
+            codes, scales = codes_of[(w, g)]
+            cols = slice(c * BLOCK, (c + 1) * BLOCK)
             nc.vector.quantize_mx(
-                out=rh_codes[:, c, :].bitcast(FP8X4),
-                scales=rh_scales[:, c, :],
-                in_=rh_grouped[:].rearrange("p b t -> p (b t)"),
+                out=codes[:, cols].bitcast(FP8X4),
+                scales=scales[:, cols],
+                in_=grouped_of[(w, g, c)][:].rearrange("p n t -> p (n t)"),
             )
 
-        def finish_gate(c, accs):
+        accs_of = {}
+
+        def bank_of(c, t):
+            return "bank%d" % (PACK * (c % 2) + t)
+
+        def passes(w, c, chunks):
+            for g in chunks:
+                codes, scales = codes_of[(w, g)]
+                for t in range(PACK):
+                    cols = slice(c * BLOCK + t * P, c * BLOCK + (t + 1) * P)
+                    nc.tensor.matmul_mx(
+                        out=accs_of[(w, c)][t][:],
+                        lhsT=codes[:, cols].bitcast(FP8X4),
+                        lhsT_scale=scales[:, cols],
+                        rhs=moving[w][g][0].bitcast(FP8X4),
+                        rhs_scale=moving[w][g][1],
+                        start=(g == 0),
+                        stop=(g == CHUNKS - 1),
+                    )
+
+        r_of = {}
+        rh_grouped_of = {}
+        out_ps_of = {}
+
+        def reset_sigmoid(c):
+            r_of[c] = work.tile([P, PACK, B], F32, name="r_sb", tag="four_tiles")
             for t in range(PACK):
                 i = c * PACK + t
                 nc.scalar.activation(
-                    out=silu_gate[:, i, :], in_=accs[t][:], func=ACT.Silu, bias=bias[:, H_TILES + i : H_TILES + i + 1]
+                    out=r_of[c][:, t, :], in_=accs_of[(0, c)][t][:], func=ACT.Sigmoid, bias=bias[:, i : i + 1]
                 )
 
-        def finish_up(c, accs):
+        def reset_times_hidden(c):
+            rh_grouped_of[c] = work.tile([P, B, PACK], BF16, name="rh_grouped", align_bytes=64)
+            nc.vector.tensor_tensor(
+                out=rh_grouped_of[c][:],
+                in0=r_of[c][:].rearrange("p t b -> p b t"),
+                in1=acts_grouped[:, c + 1, :, :],
+                op=ALU.mult,
+            )
+
+        def reset_quantise(c):
+            nc.vector.quantize_mx(
+                out=rh_codes[:, c, :].bitcast(FP8X4),
+                scales=rh_scales[:, c, :],
+                in_=rh_grouped_of[c][:].rearrange("p b t -> p (b t)"),
+            )
+
+        def gate_silu(c):
+            for t in range(PACK):
+                i = c * PACK + t
+                nc.scalar.activation(
+                    out=silu_gate[:, i, :],
+                    in_=accs_of[(1, c)][t][:],
+                    func=ACT.Silu,
+                    bias=bias[:, H_TILES + i : H_TILES + i + 1],
+                )
+
+        def up_product(c):
             product = work.tile([P, PACK, B], F32, tag="four_tiles")
             for t in range(PACK):
                 i = c * PACK + t
                 nc.vector.scalar_tensor_tensor(
                     out=product[:, t, :],
-                    in0=accs[t][:],
+                    in0=accs_of[(2, c)][t][:],
                     scalar=bias[:, 2 * H_TILES + i : 2 * H_TILES + i + 1],
                     in1=silu_gate[:, i, :],
                     op0=ALU.add,
                     op1=ALU.mult,
                 )
             for s in range(B_TILES):
-                out_ps = psum_tr.tile([P, BLOCK], F32, tag="tr")
+                out_ps_of[(c, s)] = psum.tile([P, BLOCK], F32, name="out_ps", tag=bank_of(c, s))
                 for t in range(PACK):
-                    nc.tensor.transpose(out_ps[:, t * P : (t + 1) * P], product[:, t, s * P : (s + 1) * P], ident_f32[:])
+                    nc.tensor.transpose(
+                        out_ps_of[(c, s)][:, t * P : (t + 1) * P], product[:, t, s * P : (s + 1) * P], ident_f32[:]
+                    )
+
+        def up_store(c, copies):
+            for s in range(B_TILES):
                 out_sb = stores.tile([P, BLOCK], F32)
-                if s % 2 == 0:
-                    nc.scalar.copy(out=out_sb[:], in_=out_ps[:])
-                else:
-                    nc.vector.tensor_copy(out=out_sb[:], in_=out_ps[:])
+                copies[s](out=out_sb[:], in_=out_ps_of[(c, s)][:])
                 nc.sync.dma_start(out=out[s * P : (s + 1) * P, c * BLOCK : (c + 1) * BLOCK], in_=out_sb[:])
 
-        def stream_weight(w, moving, finish_block):
-            codes = quantised.tile([P, CHUNKS, H], U32, align_bytes=64, tag="w_codes")
-            scales = quantised.tile([P, CHUNKS, H], U8, align_bytes=64, tag="w_scales")
+        def pieces_of(s):
+            w, i = divmod(s, STEPS)
+            if i < 2 * WHOLE:
+                return (w, i // 2, 2 * (i % 2)), (w, i // 2, 2 * (i % 2) + 1)
+            return (w, WHOLE, i - 2 * WHOLE), (w, WHOLE + 1, i - 2 * WHOLE)
 
-            def quantise_piece(g, c):
-                cols = slice(c * BLOCK, (c + 1) * BLOCK)
-                grouped = regroup.tile([P, BLOCK, PACK], BF16, align_bytes=64)
-                source = raw_tiles[w * CHUNKS + g][:, :, cols].rearrange("p t (n i) -> p n t i", i=RUN)
-                target = grouped[:].rearrange("p (n i) t -> p n t i", i=RUN)
-                if (g + c) % 2 == 0:
-                    nc.vector.tensor_copy(out=target, in_=source)
-                else:
-                    nc.scalar.copy(out=target, in_=source)
-                nc.vector.quantize_mx(
-                    out=codes[:, g, cols].bitcast(FP8X4),
-                    scales=scales[:, g, cols],
-                    in_=grouped[:].rearrange("p n t -> p (n t)"),
-                )
+        def block_of(s):
+            w, i = divmod(s, STEPS)
+            if 0 <= s < TOTAL_STEPS and i >= 2 * WHOLE:
+                return (w, i - 2 * WHOLE)
+            return None
 
-            def passes(c, accs, chunks):
-                for g in chunks:
-                    for t in range(PACK):
-                        cols = slice(c * BLOCK + t * P, c * BLOCK + (t + 1) * P)
-                        nc.tensor.matmul_mx(
-                            out=accs[t][:],
-                            lhsT=codes[:, g, cols].bitcast(FP8X4),
-                            lhsT_scale=scales[:, g, cols],
-                            rhs=moving[g][0].bitcast(FP8X4),
-                            rhs_scale=moving[g][1],
-                            start=(g == 0),
-                            stop=(g == CHUNKS - 1),
-                        )
+        for s in range(TOTAL_STEPS):
+            w, i = divmod(s, STEPS)
+            first, second = pieces_of(s)
+            summed = block_of(s - 2)
+            summed_w, summed_c = summed if summed is not None else (None, None)
+            if summed_w == 0:
+                reset_sigmoid(summed_c)
+            if summed_w == 1:
+                gate_silu(summed_c)
+            if summed_w == 2:
+                up_product(summed_c)
+            scalar_from = BLOCK // 2 if summed_w == 1 else 0
+            regroup_columns(nc.vector.tensor_copy, *first, 0, BLOCK)
+            if scalar_from > 0:
+                regroup_columns(nc.vector.tensor_copy, *second, 0, scalar_from)
+            regroup_columns(nc.scalar.copy, *second, scalar_from, BLOCK)
+            if s >= 1:
+                quantise_piece(*pieces_of(s - 1)[1])
+            if block_of(s - 1) is not None:
+                passes(*block_of(s - 1), [CHUNKS - 1])
+            if summed_w == 0:
+                reset_times_hidden(summed_c)
+            quantise_piece(*first)
+            if summed_w == 0:
+                reset_quantise(summed_c)
+            if summed_w == 2:
+                up_store(summed_c, [nc.scalar.copy, nc.scalar.copy])
+            if block_of(s) is not None:
+                c = block_of(s)[1]
+                accs_of[(w, c)] = [psum.tile([P, B], F32, name="acc", tag=bank_of(c, t)) for t in range(PACK)]
+                passes(w, c, range(CHUNKS - 1))
+            if i < 2 * WHOLE and i % 2 == 1:
+                load_whole(w + 1, i // 2)
+            if i == STEPS - 1:
+                load_pair(w + 1)
+            if s == 1:
+                transpose_activations()
+            if 1 <= s <= CHUNKS:
+                copy_activations(s - 1)
+            if 2 <= s <= CHUNKS + 1:
+                quantise_activations(s - 2)
+            if s == CHUNKS + 1:
+                nc.vector.tensor_copy(out=bias[:], in_=acts_ps[CHUNKS][:])
+                nc.vector.tensor_copy(out=bias[:, 0:H_TILES], in_=b_r_sb[:].rearrange("p c t -> p (c t)"))
 
-            last = CHUNKS - 1
-            for g in range(last):
-                for c in range(BLOCKS):
-                    quantise_piece(g, c)
-                load_next_chunk()
-                if w == 0 and g == 0:
-                    prepare_activations()
-                    load_next_chunk()
-            for c in range(BLOCKS):
-                accs = [psum_acc.tile([P, B], F32, name="acc", tag="acc") for t in range(PACK)]
-                passes(c, accs, range(last))
-                quantise_piece(last, c)
-                passes(c, accs, [last])
-                finish_block(c, accs)
-            load_next_chunk()
-
-        stream_weight(0, x_and_h, finish_reset)
-        stream_weight(1, x_and_rh, finish_gate)
-        stream_weight(2, x_and_rh, finish_up)
+        quantise_piece(*pieces_of(TOTAL_STEPS - 1)[1])
+        passes(WEIGHTS - 1, BLOCKS - 1, [CHUNKS - 1])
+        up_product(BLOCKS - 2)
+        up_store(BLOCKS - 2, [nc.scalar.copy, nc.scalar.copy])
+        up_product(BLOCKS - 1)
+        up_store(BLOCKS - 1, [nc.scalar.copy, nc.vector.tensor_copy])

@@ -24,10 +24,11 @@ H_TILES = H // P
 B_TILES = B // P
 RUN = 4
 WEIGHTS = 3
-WHOLE = CHUNKS - 2
-STEPS = CHUNKS * BLOCKS // 2
-TOTAL_STEPS = WEIGHTS * STEPS
-BANKS = 8
+HALF = 2 * BLOCK
+HALVES = H // HALF
+STEPS = WEIGHTS * HALVES * CHUNKS
+RAW_BUFS = 8
+CODE_BUFS = 6
 
 FLOPS = 2 * B * C * H * 3
 
@@ -37,59 +38,52 @@ def tile_recurrentffn_pa_kernel(tc, x, hidden_state, W_r, b_r, W_g, b_g, W_up, b
     weights = [W_r, W_g, W_up]
     with ExitStack() as ctx:
         const = ctx.enter_context(tc.tile_pool(name="const", bufs=1))
-        staging_whole = ctx.enter_context(tc.tile_pool(name="staging_whole", bufs=WHOLE))
-        staging_pair = ctx.enter_context(tc.tile_pool(name="staging_pair", bufs=1))
+        staging = ctx.enter_context(tc.tile_pool(name="staging", bufs=RAW_BUFS))
         regroup = ctx.enter_context(tc.tile_pool(name="regroup", bufs=4))
-        quantised = ctx.enter_context(tc.tile_pool(name="quantised", bufs=CHUNKS + 1))
+        quantised = ctx.enter_context(tc.tile_pool(name="quantised", bufs=CODE_BUFS))
         work = ctx.enter_context(tc.tile_pool(name="work", bufs=2))
         stores = ctx.enter_context(tc.tile_pool(name="stores", bufs=4))
         psum = ctx.enter_context(tc.psum_pool(name="psum", bufs=1))
         ctx.enter_context(tc.manual_schedule())
 
-        whole_tiles = {}
-        pair_tiles = {}
-
-        def rows_of(w, g):
-            return weights[w][g * K_PASS : (g + 1) * K_PASS, :].rearrange("(p t) n -> p t n", t=PACK)
-
-        def load_whole(w, g):
-            if w >= WEIGHTS:
-                return
-            raw = staging_whole.tile([P, PACK, H], BF16, tag="whole")
-            width = 2 * BLOCK if w == 0 else H
-            for n0 in range(0, H, width):
-                nc.sync.dma_start(out=raw[:, :, n0 : n0 + width], in_=rows_of(w, g)[:, :, n0 : n0 + width])
-            whole_tiles[(w, g)] = raw
-
-        def load_pair(w):
-            if w >= WEIGHTS:
-                return
-            raw = staging_pair.tile([P, 2, PACK, H], BF16, tag="pair")
-            width = BLOCK if w == 0 else H
-            for n0 in range(0, H, width):
-                for j in range(2):
-                    nc.sync.dma_start(
-                        out=raw[:, j, :, n0 : n0 + width], in_=rows_of(w, WHOLE + j)[:, :, n0 : n0 + width]
-                    )
-            pair_tiles[w] = raw
+        def place_of(s):
+            return s // (HALVES * CHUNKS), (s // CHUNKS) % HALVES, s % CHUNKS
 
         b_r_sb = const.tile([P, BLOCKS, PACK], BF16)
         nc.scalar.dma_start(out=b_r_sb[:], in_=b_r.rearrange("(c p t) -> p c t", p=P, t=PACK))
         bias_rows = const.tile([P, P], BF16)
-        nc.vector.memset(bias_rows[:], 0.0)
         for w, b in [(1, b_g), (2, b_up)]:
             nc.scalar.dma_start(
-                out=bias_rows[w * H_TILES : (w + 1) * H_TILES, :],
+                out=bias_rows[(w - 1) * H_TILES : w * H_TILES, :],
                 in_=b.rearrange("(i p) -> i p", p=P),
             )
+        nc.vector.memset(bias_rows[2 * H_TILES : 4 * H_TILES, :], 0.0)
+        nc.vector.memset(bias_rows[4 * H_TILES : P, :], 0.0)
 
-        load_whole(0, 0)
         acts_sb = const.tile([P, B_TILES, C], BF16)
         nc.sync.dma_start(out=acts_sb[:, :, 0:D], in_=x.rearrange("(s p) d -> p s d", p=P))
-        nc.sync.dma_start(out=acts_sb[:, :, D:C], in_=hidden_state.rearrange("(s p) d -> p s d", p=P))
-        for g in range(1, WHOLE):
-            load_whole(0, g)
-        load_pair(0)
+        for k0 in range(D, C, H // 2):
+            nc.sync.dma_start(
+                out=acts_sb[:, :, k0 : k0 + H // 2],
+                in_=hidden_state[:, k0 - D : k0 - D + H // 2].rearrange("(s p) d -> p s d", p=P),
+            )
+
+        raw_of = {}
+
+        def load_step(s):
+            if s >= STEPS:
+                return
+            w, h, g = place_of(s)
+            raw_of[s] = staging.tile([P, PACK, HALF], BF16, name="raw")
+            nc.sync.dma_start(
+                out=raw_of[s][:],
+                in_=weights[w][g * K_PASS : (g + 1) * K_PASS, h * HALF : (h + 1) * HALF].rearrange(
+                    "(p t) n -> p t n", t=PACK
+                ),
+            )
+
+        for s in range(RAW_BUFS):
+            load_step(s)
 
         ident_bf = const.tile([P, P], BF16)
         make_identity(nc, ident_bf[:])
@@ -98,46 +92,42 @@ def tile_recurrentffn_pa_kernel(tc, x, hidden_state, W_r, b_r, W_g, b_g, W_up, b
 
         zero = const.tile([P, 1], F32)
         nc.vector.memset(zero[:], 0.0)
-        half = const.tile([P, 1], F32)
-        nc.scalar.activation(out=half[:], in_=zero[:], func=ACT.Sigmoid)
+        half_one = const.tile([P, 1], F32)
+        nc.scalar.activation(out=half_one[:], in_=zero[:], func=ACT.Sigmoid)
 
         bias = const.tile([P, P], F32)
+        bias_ps = psum.tile([P, P], BF16, tag="bank%d" % CHUNKS)
+        nc.tensor.transpose(bias_ps[:], bias_rows[:], ident_bf[:])
+        nc.vector.tensor_copy(out=bias[:], in_=bias_ps[:])
+        nc.vector.tensor_copy(out=bias[:, 2 * H_TILES : 3 * H_TILES], in_=b_r_sb[:].rearrange("p c t -> p (c t)"))
+        bias_of = [bias[:, 2 * H_TILES : 3 * H_TILES], bias[:, 0:H_TILES], bias[:, H_TILES : 2 * H_TILES]]
 
         acts_grouped = const.tile([P, CHUNKS, B, PACK], BF16, align_bytes=64)
         acts_codes = const.tile([P, CHUNKS, B], U32, align_bytes=64)
         acts_scales = const.tile([P, CHUNKS, B], U8, align_bytes=64)
-        rh_codes = const.tile([P, BLOCKS, B], U32, align_bytes=64)
-        rh_scales = const.tile([P, BLOCKS, B], U8, align_bytes=64)
-        silu_gate = const.tile([P, H_TILES, B], F32)
-
-        acts_ps = {}
-
-        def transpose_activations():
-            for g in range(CHUNKS):
-                acts_ps[g] = psum.tile([P, 2, B], F32, name="acts_ps", tag="bank%d" % g)
-                for u in range(2):
-                    for s in range(B_TILES):
-                        words = acts_sb[:, s, g * K_PASS : (g + 1) * K_PASS].bitcast(F32)
-                        nc.tensor.transpose(
-                            acts_ps[g][:, u, s * P : (s + 1) * P],
-                            words.rearrange("p (j u) -> p j u", u=2)[:, :, u],
-                            ident_f32[:],
-                        )
-            acts_ps[CHUNKS] = psum.tile([P, P], BF16, name="bias_ps", tag="bank%d" % CHUNKS)
-            nc.tensor.transpose(acts_ps[CHUNKS][:], bias_rows[:], ident_bf[:])
-
-        def copy_activations(g):
+        for g in range(CHUNKS):
+            acts_ps = psum.tile([P, 2, B], F32, tag="bank%d" % g)
+            for u in range(2):
+                for s in range(B_TILES):
+                    words = acts_sb[:, s, g * K_PASS : (g + 1) * K_PASS].bitcast(F32)
+                    nc.tensor.transpose(
+                        acts_ps[:, u, s * P : (s + 1) * P],
+                        words.rearrange("p (j u) -> p j u", u=2)[:, :, u],
+                        ident_f32[:],
+                    )
             nc.scalar.copy(
                 out=acts_grouped[:, g, :, :].rearrange("p b t -> p (b t)").bitcast(F32).rearrange("p (b u) -> p b u", u=2),
-                in_=acts_ps[g][:].rearrange("p u b -> p b u"),
+                in_=acts_ps[:].rearrange("p u b -> p b u"),
             )
-
-        def quantise_activations(g):
             nc.vector.quantize_mx(
                 out=acts_codes[:, g, :].bitcast(FP8X4),
                 scales=acts_scales[:, g, :],
                 in_=acts_grouped[:, g, :, :].rearrange("p b t -> p (b t)"),
             )
+
+        rh_codes = const.tile([P, BLOCKS, B], U32, align_bytes=64)
+        rh_scales = const.tile([P, BLOCKS, B], U8, align_bytes=64)
+        silu_gate = const.tile([P, H_TILES, B], F32)
 
         x_and_h = [(acts_codes[:, g, :], acts_scales[:, g, :]) for g in range(CHUNKS)]
         x_and_rh = x_and_h[0:1] + [(rh_codes[:, c, :], rh_scales[:, c, :]) for c in range(BLOCKS)]
@@ -145,43 +135,43 @@ def tile_recurrentffn_pa_kernel(tc, x, hidden_state, W_r, b_r, W_g, b_g, W_up, b
 
         grouped_of = {}
         codes_of = {}
-
-        def regroup_columns(copy, w, g, c, n0, n1):
-            if n0 == 0:
-                grouped_of[(w, g, c)] = regroup.tile([P, BLOCK, PACK], BF16, name="grouped", align_bytes=64)
-            raw = whole_tiles[(w, g)] if g < WHOLE else pair_tiles[w][:, g - WHOLE]
-            assert w > 0 or (n0, n1) == (0, BLOCK)
-            places = "p (i n) t -> p n t i" if w == 0 else "p (n i) t -> p n t i"
-            copy(
-                out=grouped_of[(w, g, c)][:, n0:n1, :].rearrange(places, i=RUN),
-                in_=raw[:, :, c * BLOCK + n0 : c * BLOCK + n1].rearrange("p t (n i) -> p n t i", i=RUN),
-            )
-
-        def quantise_piece(w, g, c):
-            if c == 0:
-                codes = quantised.tile([P, H], U32, align_bytes=64, tag="w_codes")
-                scales = quantised.tile([P, H], U8, align_bytes=64, tag="w_scales")
-                codes_of[(w, g)] = (codes, scales)
-            codes, scales = codes_of[(w, g)]
-            cols = slice(c * BLOCK, (c + 1) * BLOCK)
-            nc.vector.quantize_mx(
-                out=codes[:, cols].bitcast(FP8X4),
-                scales=scales[:, cols],
-                in_=grouped_of[(w, g, c)][:].rearrange("p n t -> p (n t)"),
-            )
-
         accs_of = {}
 
-        def bank_of(c, t):
-            return "bank%d" % (PACK * (c % 2) + t)
+        def regroup_piece(copy, s, j):
+            grouped_of[(s, j)] = regroup.tile([P, BLOCK, PACK], BF16, name="grouped", align_bytes=64)
+            places = "p (i n) t -> p n t i" if place_of(s)[0] == 0 else "p (n i) t -> p n t i"
+            copy(
+                out=grouped_of[(s, j)][:].rearrange(places, i=RUN),
+                in_=raw_of[s][:, :, j * BLOCK : (j + 1) * BLOCK].rearrange("p t (n i) -> p n t i", i=RUN),
+            )
 
-        def passes(w, c, chunks):
-            for g in chunks:
-                codes, scales = codes_of[(w, g)]
+        def quantise_piece(s, j):
+            if j == 0:
+                codes = quantised.tile([P, HALF], U32, align_bytes=64)
+                scales = quantised.tile([P, HALF], U8, align_bytes=64)
+                codes_of[s] = (codes, scales)
+            codes, scales = codes_of[s]
+            nc.vector.quantize_mx(
+                out=codes[:, j * BLOCK : (j + 1) * BLOCK].bitcast(FP8X4),
+                scales=scales[:, j * BLOCK : (j + 1) * BLOCK],
+                in_=grouped_of[(s, j)][:].rearrange("p n t -> p (n t)"),
+            )
+
+        def bank_of(j, t):
+            return "bank%d" % (PACK * j + t)
+
+        def passes(s):
+            w, h, g = place_of(s)
+            codes, scales = codes_of[s]
+            for j in range(2):
+                if g == 0:
+                    accs_of[(w, 2 * h + j)] = [
+                        psum.tile([P, B], F32, name="acc", tag=bank_of(j, t)) for t in range(PACK)
+                    ]
                 for t in range(PACK):
-                    cols = slice(c * BLOCK + t * P, c * BLOCK + (t + 1) * P)
+                    cols = slice(j * BLOCK + t * P, j * BLOCK + (t + 1) * P)
                     nc.tensor.matmul_mx(
-                        out=accs_of[(w, c)][t][:],
+                        out=accs_of[(w, 2 * h + j)][t][:],
                         lhsT=codes[:, cols].bitcast(FP8X4),
                         lhsT_scale=scales[:, cols],
                         rhs=moving[w][g][0].bitcast(FP8X4),
@@ -199,7 +189,7 @@ def tile_recurrentffn_pa_kernel(tc, x, hidden_state, W_r, b_r, W_g, b_g, W_up, b
             for t in range(PACK):
                 i = c * PACK + t
                 nc.scalar.activation(
-                    out=r_of[c][:, t, :], in_=accs_of[(0, c)][t][:], func=ACT.Sigmoid, bias=bias[:, i : i + 1]
+                    out=r_of[c][:, t, :], in_=accs_of[(0, c)][t][:], func=ACT.Sigmoid, bias=bias_of[0][:, i : i + 1]
                 )
 
         def reset_times_hidden(c):
@@ -225,7 +215,7 @@ def tile_recurrentffn_pa_kernel(tc, x, hidden_state, W_r, b_r, W_g, b_g, W_up, b
                     out=silu_gate[:, i, :],
                     in_=accs_of[(1, c)][t][:],
                     func=ACT.Silu,
-                    bias=bias[:, H_TILES + i : H_TILES + i + 1],
+                    bias=bias_of[1][:, i : i + 1],
                 )
 
         def up_product(c):
@@ -235,13 +225,13 @@ def tile_recurrentffn_pa_kernel(tc, x, hidden_state, W_r, b_r, W_g, b_g, W_up, b
                 nc.vector.scalar_tensor_tensor(
                     out=product[:, t, :],
                     in0=accs_of[(2, c)][t][:],
-                    scalar=bias[:, 2 * H_TILES + i : 2 * H_TILES + i + 1],
+                    scalar=bias_of[2][:, i : i + 1],
                     in1=silu_gate[:, i, :],
                     op0=ALU.add,
                     op1=ALU.mult,
                 )
             for s in range(B_TILES):
-                out_ps_of[(c, s)] = psum.tile([P, BLOCK], F32, name="out_ps", tag=bank_of(c, s))
+                out_ps_of[(c, s)] = psum.tile([P, BLOCK], F32, name="out_ps", tag=bank_of(c % 2, s))
                 for t in range(PACK):
                     nc.tensor.transpose(
                         out_ps_of[(c, s)][:, t * P : (t + 1) * P], product[:, t, s * P : (s + 1) * P], ident_f32[:]
@@ -253,66 +243,37 @@ def tile_recurrentffn_pa_kernel(tc, x, hidden_state, W_r, b_r, W_g, b_g, W_up, b
                 copies[s](out=out_sb[:], in_=out_ps_of[(c, s)][:])
                 nc.sync.dma_start(out=out[s * P : (s + 1) * P, c * BLOCK : (c + 1) * BLOCK], in_=out_sb[:])
 
-        def pieces_of(s):
-            w, i = divmod(s, STEPS)
-            if i < 2 * WHOLE:
-                return (w, i // 2, 2 * (i % 2)), (w, i // 2, 2 * (i % 2) + 1)
-            return (w, WHOLE, i - 2 * WHOLE), (w, WHOLE + 1, i - 2 * WHOLE)
-
-        def block_of(s):
-            w, i = divmod(s, STEPS)
-            if 0 <= s < TOTAL_STEPS and i >= 2 * WHOLE:
-                return (w, i - 2 * WHOLE)
-            return None
-
-        for s in range(TOTAL_STEPS):
-            w, i = divmod(s, STEPS)
-            first, second = pieces_of(s)
-            summed = block_of(s - 2)
-            summed_w, summed_c = summed if summed is not None else (None, None)
-            if summed_w == 0:
-                reset_sigmoid(summed_c)
-            if summed_w == 1:
-                gate_silu(summed_c)
-            if summed_w == 2:
-                up_product(summed_c)
-            scalar_from = BLOCK // 2 if summed_w == 1 else 0
-            regroup_columns(nc.vector.tensor_copy, *first, 0, BLOCK)
-            if scalar_from > 0:
-                regroup_columns(nc.vector.tensor_copy, *second, 0, scalar_from)
-            regroup_columns(nc.scalar.copy, *second, scalar_from, BLOCK)
-            if s >= 1:
-                quantise_piece(*pieces_of(s - 1)[1])
-            if block_of(s - 1) is not None:
-                passes(*block_of(s - 1), [CHUNKS - 1])
-            if summed_w == 0:
-                reset_times_hidden(summed_c)
-            quantise_piece(*first)
-            if summed_w == 0:
-                reset_quantise(summed_c)
-            if summed_w == 2:
-                up_store(summed_c, [nc.scalar.copy, nc.scalar.copy])
-            if block_of(s) is not None:
-                c = block_of(s)[1]
-                accs_of[(w, c)] = [psum.tile([P, B], F32, name="acc", tag=bank_of(c, t)) for t in range(PACK)]
-                passes(w, c, range(CHUNKS - 1))
-            if i < 2 * WHOLE and i % 2 == 1:
-                load_whole(w + 1, i // 2)
-            if i == STEPS - 1:
-                load_pair(w + 1)
-            if s == 1:
-                transpose_activations()
-            if 1 <= s <= CHUNKS:
-                copy_activations(s - 1)
-            if 2 <= s <= CHUNKS + 1:
-                quantise_activations(s - 2)
-            if s == CHUNKS + 1:
-                nc.vector.tensor_copy(out=bias[:], in_=acts_ps[CHUNKS][:])
-                nc.vector.tensor_copy(out=bias[:, 0:H_TILES], in_=b_r_sb[:].rearrange("p c t -> p (c t)"))
-
-        quantise_piece(*pieces_of(TOTAL_STEPS - 1)[1])
-        passes(WEIGHTS - 1, BLOCKS - 1, [CHUNKS - 1])
-        up_product(BLOCKS - 2)
-        up_store(BLOCKS - 2, [nc.scalar.copy, nc.scalar.copy])
-        up_product(BLOCKS - 1)
-        up_store(BLOCKS - 1, [nc.scalar.copy, nc.vector.tensor_copy])
+        for s in range(STEPS + 2):
+            finish_w, finish_h, finish_g = place_of(s - 2) if s >= 2 else (None, None, None)
+            if finish_g != CHUNKS - 1:
+                finish_w = None
+            first_c = 2 * finish_h if finish_w is not None else None
+            if finish_w == 0:
+                reset_sigmoid(first_c)
+                reset_sigmoid(first_c + 1)
+            if finish_w == 1:
+                gate_silu(first_c)
+                gate_silu(first_c + 1)
+            if finish_w == 2:
+                up_product(first_c)
+                up_product(first_c + 1)
+            if s < STEPS:
+                regroup_piece(nc.vector.tensor_copy, s, 0)
+                regroup_piece(nc.vector.tensor_copy if finish_w == 1 else nc.scalar.copy, s, 1)
+            if 1 <= s <= STEPS:
+                quantise_piece(s - 1, 1)
+            if finish_w == 0:
+                reset_times_hidden(first_c)
+            if s < STEPS:
+                quantise_piece(s, 0)
+            if finish_w == 0:
+                reset_times_hidden(first_c + 1)
+                reset_quantise(first_c)
+                reset_quantise(first_c + 1)
+            if finish_w == 2:
+                last = s == STEPS + 1
+                up_store(first_c, [nc.scalar.copy, nc.scalar.copy])
+                up_store(first_c + 1, [nc.scalar.copy, nc.vector.tensor_copy if last else nc.scalar.copy])
+            if 1 <= s <= STEPS:
+                passes(s - 1)
+            load_step(s + RAW_BUFS)

@@ -28,8 +28,21 @@ HALF = 2 * BLOCK
 HALVES = H // HALF
 STEPS = WEIGHTS * HALVES * CHUNKS
 RAW_BUFS = 8
-CODE_BUFS = 6
+GROUP_BUFS = 4
+CODE_BUFS = 8
+LQ = 1
+LAG_FIRST = 1
+LAG_SECOND = 2
+RH_LAG = 1
+STORE_LAG = 1
+SHARES = {1: 640}
+LAST_BY_BLOCKS = True
+SHARE_NORMAL = 496
+SHARE_SILU = 640
+SHARE_ROUTE = 336
+ROUTE_CHUNKS = ()
 
+OUT_BANKS = [6, 4, 0, 4]
 FLOPS = 2 * B * C * H * 3
 
 
@@ -39,7 +52,7 @@ def tile_recurrentffn_pa_kernel(tc, x, hidden_state, W_r, b_r, W_g, b_g, W_up, b
     with ExitStack() as ctx:
         const = ctx.enter_context(tc.tile_pool(name="const", bufs=1))
         staging = ctx.enter_context(tc.tile_pool(name="staging", bufs=RAW_BUFS))
-        regroup = ctx.enter_context(tc.tile_pool(name="regroup", bufs=4))
+        regroup = ctx.enter_context(tc.tile_pool(name="regroup", bufs=GROUP_BUFS))
         quantised = ctx.enter_context(tc.tile_pool(name="quantised", bufs=CODE_BUFS))
         work = ctx.enter_context(tc.tile_pool(name="work", bufs=2))
         stores = ctx.enter_context(tc.tile_pool(name="stores", bufs=4))
@@ -48,6 +61,37 @@ def tile_recurrentffn_pa_kernel(tc, x, hidden_state, W_r, b_r, W_g, b_g, W_up, b
 
         def place_of(s):
             return s // (HALVES * CHUNKS), (s // CHUNKS) % HALVES, s % CHUNKS
+
+        units = [[(s, 0), (s, 1)] for s in range(STEPS)]
+        if LAST_BY_BLOCKS:
+            last_half = [(STEPS - CHUNKS + g, j) for j in range(2) for g in range(CHUNKS)]
+            for k in range(CHUNKS):
+                units[STEPS - CHUNKS + k] = last_half[2 * k : 2 * k + 2]
+        route_units = [u for u in range(1, STEPS - CHUNKS) if u % CHUNKS in ROUTE_CHUNKS]
+
+        def shares_banks(w, c):
+            return c % 2 == 1 and (w, c) != (WEIGHTS - 1, BLOCKS - 1)
+
+        def pair_banks(w, c):
+            return PACK + 2 * ((w * HALVES + c // 2) % 2)
+
+        act_part = {}
+        dve_part = {}
+        store_part = {}
+        for u in range(STEPS):
+            for step, j in units[u]:
+                w, h, g = place_of(step)
+                c = 2 * h + j
+                if g == CHUNKS - 1:
+                    at = u + LQ + (LAG_SECOND if shares_banks(w, c) else LAG_FIRST)
+                    if w == 0:
+                        act_part.setdefault(at, []).append((w, c))
+                        dve_part.setdefault(at + RH_LAG, []).append((w, c))
+                    if w == 1:
+                        act_part.setdefault(at, []).append((w, c))
+                    if w == 2:
+                        dve_part.setdefault(at, []).append((w, c))
+                        store_part.setdefault(at + (0 if c == BLOCKS - 1 else STORE_LAG), []).append((w, c))
 
         b_r_sb = const.tile([P, BLOCKS, PACK], BF16)
         nc.scalar.dma_start(out=b_r_sb[:], in_=b_r.rearrange("(c p t) -> p c t", p=P, t=PACK))
@@ -60,29 +104,36 @@ def tile_recurrentffn_pa_kernel(tc, x, hidden_state, W_r, b_r, W_g, b_g, W_up, b
         nc.vector.memset(bias_rows[2 * H_TILES : 4 * H_TILES, :], 0.0)
         nc.vector.memset(bias_rows[4 * H_TILES : P, :], 0.0)
 
-        acts_sb = const.tile([P, B_TILES, C], BF16)
-        nc.sync.dma_start(out=acts_sb[:, :, 0:D], in_=x.rearrange("(s p) d -> p s d", p=P))
-        for k0 in range(D, C, H // 2):
-            nc.sync.dma_start(
-                out=acts_sb[:, :, k0 : k0 + H // 2],
-                in_=hidden_state[:, k0 - D : k0 - D + H // 2].rearrange("(s p) d -> p s d", p=P),
-            )
-
         raw_of = {}
 
-        def load_step(s):
+        def load_step(s, parts=1):
             if s >= STEPS:
                 return
             w, h, g = place_of(s)
             raw_of[s] = staging.tile([P, PACK, HALF], BF16, name="raw")
-            nc.sync.dma_start(
-                out=raw_of[s][:],
-                in_=weights[w][g * K_PASS : (g + 1) * K_PASS, h * HALF : (h + 1) * HALF].rearrange(
-                    "(p t) n -> p t n", t=PACK
-                ),
-            )
+            width = HALF // parts
+            for k in range(parts):
+                nc.sync.dma_start(
+                    out=raw_of[s][:, :, k * width : (k + 1) * width],
+                    in_=weights[w][
+                        g * K_PASS : (g + 1) * K_PASS, h * HALF + k * width : h * HALF + (k + 1) * width
+                    ].rearrange("(p t) n -> p t n", t=PACK),
+                )
 
-        for s in range(RAW_BUFS):
+        acts_sb = const.tile([P, B_TILES, C], BF16)
+
+        def load_acts():
+            nc.sync.dma_start(out=acts_sb[:, :, 0:D], in_=x.rearrange("(s p) d -> p s d", p=P))
+            for k0 in range(D, C, H // 2):
+                nc.sync.dma_start(
+                    out=acts_sb[:, :, k0 : k0 + H // 2],
+                    in_=hidden_state[:, k0 - D : k0 - D + H // 2].rearrange("(s p) d -> p s d", p=P),
+                )
+
+        load_step(0, 2)
+        load_step(1)
+        load_acts()
+        for s in range(2, RAW_BUFS):
             load_step(s)
 
         ident_bf = const.tile([P, P], BF16)
@@ -96,33 +147,39 @@ def tile_recurrentffn_pa_kernel(tc, x, hidden_state, W_r, b_r, W_g, b_g, W_up, b
         nc.scalar.activation(out=half_one[:], in_=zero[:], func=ACT.Sigmoid)
 
         bias = const.tile([P, P], F32)
-        bias_ps = psum.tile([P, P], BF16, tag="bank%d" % CHUNKS)
-        nc.tensor.transpose(bias_ps[:], bias_rows[:], ident_bf[:])
-        nc.vector.tensor_copy(out=bias[:], in_=bias_ps[:])
-        nc.vector.tensor_copy(out=bias[:, 2 * H_TILES : 3 * H_TILES], in_=b_r_sb[:].rearrange("p c t -> p (c t)"))
         bias_of = [bias[:, 2 * H_TILES : 3 * H_TILES], bias[:, 0:H_TILES], bias[:, H_TILES : 2 * H_TILES]]
-
         acts_grouped = const.tile([P, CHUNKS, B, PACK], BF16, align_bytes=64)
         acts_codes = const.tile([P, CHUNKS, B], U32, align_bytes=64)
         acts_scales = const.tile([P, CHUNKS, B], U8, align_bytes=64)
-        for g in range(CHUNKS):
-            acts_ps = psum.tile([P, 2, B], F32, tag="bank%d" % g)
-            for u in range(2):
-                for s in range(B_TILES):
-                    words = acts_sb[:, s, g * K_PASS : (g + 1) * K_PASS].bitcast(F32)
-                    nc.tensor.transpose(
-                        acts_ps[:, u, s * P : (s + 1) * P],
-                        words.rearrange("p (j u) -> p j u", u=2)[:, :, u],
-                        ident_f32[:],
-                    )
-            nc.scalar.copy(
-                out=acts_grouped[:, g, :, :].rearrange("p b t -> p (b t)").bitcast(F32).rearrange("p (b u) -> p b u", u=2),
-                in_=acts_ps[:].rearrange("p u b -> p b u"),
-            )
-            nc.vector.quantize_mx(
-                out=acts_codes[:, g, :].bitcast(FP8X4),
-                scales=acts_scales[:, g, :],
-                in_=acts_grouped[:, g, :, :].rearrange("p b t -> p (b t)"),
+
+        def prepare_acts():
+            for g in range(CHUNKS):
+                acts_ps = psum.tile([P, 2, B], F32, tag="bank%d" % g)
+                for u in range(2):
+                    for s in range(B_TILES):
+                        words = acts_sb[:, s, g * K_PASS : (g + 1) * K_PASS].bitcast(F32)
+                        nc.tensor.transpose(
+                            acts_ps[:, u, s * P : (s + 1) * P],
+                            words.rearrange("p (j u) -> p j u", u=2)[:, :, u],
+                            ident_f32[:],
+                        )
+                nc.scalar.copy(
+                    out=acts_grouped[:, g, :, :]
+                    .rearrange("p b t -> p (b t)")
+                    .bitcast(F32)
+                    .rearrange("p (b u) -> p b u", u=2),
+                    in_=acts_ps[:].rearrange("p u b -> p b u"),
+                )
+                nc.vector.quantize_mx(
+                    out=acts_codes[:, g, :].bitcast(FP8X4),
+                    scales=acts_scales[:, g, :],
+                    in_=acts_grouped[:, g, :, :].rearrange("p b t -> p (b t)"),
+                )
+            bias_ps = psum.tile([P, P], BF16, tag="bank%d" % CHUNKS)
+            nc.tensor.transpose(bias_ps[:], bias_rows[:], ident_bf[:])
+            nc.vector.tensor_copy(out=bias[:], in_=bias_ps[:])
+            nc.vector.tensor_copy(
+                out=bias[:, 2 * H_TILES : 3 * H_TILES], in_=b_r_sb[:].rearrange("p c t -> p (c t)")
             )
 
         rh_codes = const.tile([P, BLOCKS, B], U32, align_bytes=64)
@@ -136,49 +193,110 @@ def tile_recurrentffn_pa_kernel(tc, x, hidden_state, W_r, b_r, W_g, b_g, W_up, b
         grouped_of = {}
         codes_of = {}
         accs_of = {}
+        held = {}
+        passed_of = {}
 
-        def regroup_piece(copy, s, j):
-            grouped_of[(s, j)] = regroup.tile([P, BLOCK, PACK], BF16, name="grouped", align_bytes=64)
-            places = "p (i n) t -> p n t i" if place_of(s)[0] == 0 else "p (n i) t -> p n t i"
-            copy(
-                out=grouped_of[(s, j)][:].rearrange(places, i=RUN),
-                in_=raw_of[s][:, :, j * BLOCK : (j + 1) * BLOCK].rearrange("p t (n i) -> p n t i", i=RUN),
-            )
+        def regroup_cols(copy, u, lo, hi):
+            (step0, j0), (step1, j1) = units[u]
+            in_order = place_of(step0)[0] != 0
+            if in_order and step0 == step1 and lo < hi:
+                copy(
+                    out=grouped_of[u][:, lo:hi, :].rearrange("p (n i) t -> p n t i", i=RUN),
+                    in_=raw_of[step0][:, :, lo:hi].rearrange("p t (n i) -> p n t i", i=RUN),
+                )
+                return
+            for k, (step, j) in enumerate(units[u]):
+                a = max(lo, k * BLOCK) - k * BLOCK
+                b = min(hi, (k + 1) * BLOCK) - k * BLOCK
+                if a >= b:
+                    continue
+                piece = grouped_of[u][:, k * BLOCK : (k + 1) * BLOCK, :]
+                if in_order:
+                    places = piece[:, a:b, :].rearrange("p (n i) t -> p n t i", i=RUN)
+                else:
+                    places = piece.rearrange("p (i n) t -> p n t i", i=RUN)[:, a // RUN : b // RUN, :, :]
+                copy(
+                    out=places,
+                    in_=raw_of[step][:, :, j * BLOCK + a : j * BLOCK + b].rearrange("p t (n i) -> p n t i", i=RUN),
+                )
 
-        def quantise_piece(s, j):
-            if j == 0:
-                codes = quantised.tile([P, HALF], U32, align_bytes=64)
-                scales = quantised.tile([P, HALF], U8, align_bytes=64)
-                codes_of[s] = (codes, scales)
-            codes, scales = codes_of[s]
-            nc.vector.quantize_mx(
-                out=codes[:, j * BLOCK : (j + 1) * BLOCK].bitcast(FP8X4),
-                scales=scales[:, j * BLOCK : (j + 1) * BLOCK],
-                in_=grouped_of[(s, j)][:].rearrange("p n t -> p (n t)"),
-            )
-
-        def bank_of(j, t):
-            return "bank%d" % (PACK * j + t)
-
-        def passes(s):
-            w, h, g = place_of(s)
-            codes, scales = codes_of[s]
-            for j in range(2):
-                if g == 0:
-                    accs_of[(w, 2 * h + j)] = [
-                        psum.tile([P, B], F32, name="acc", tag=bank_of(j, t)) for t in range(PACK)
-                    ]
-                for t in range(PACK):
-                    cols = slice(j * BLOCK + t * P, j * BLOCK + (t + 1) * P)
-                    nc.tensor.matmul_mx(
-                        out=accs_of[(w, 2 * h + j)][t][:],
-                        lhsT=codes[:, cols].bitcast(FP8X4),
-                        lhsT_scale=scales[:, cols],
-                        rhs=moving[w][g][0].bitcast(FP8X4),
-                        rhs_scale=moving[w][g][1],
-                        start=(g == 0),
-                        stop=(g == CHUNKS - 1),
+        def pass_through(u):
+            step, j = units[u][1]
+            in_order = place_of(step)[0] != 0
+            cols = raw_of[step][:, :, j * BLOCK : (j + 1) * BLOCK]
+            view = cols.rearrange("p t (i n) -> p i n t" if in_order else "p t (n i) -> p i n t", i=PACK)
+            passed_of[u] = []
+            w, h, g = place_of(step)
+            free_pair = pair_banks(w, 2 * h + j) if g == 0 else PACK + 2 - (pair_banks(w, 2 * h + j) - PACK)
+            for q in range(2):
+                passed = psum.tile([P, 2, P, PACK], BF16, name="passed", tag="bank%d" % (free_pair + q))
+                passed_of[u].append(passed)
+                for e in range(2):
+                    nc.tensor.matmul(
+                        out=passed[:, e, :, :], lhsT=ident_bf[:], rhs=view[:, 2 * q + e, :, :], start=True, stop=True
                     )
+
+        def copy_passed(u):
+            for q in range(2):
+                nc.scalar.copy(
+                    out=grouped_of[u][:, BLOCK + 2 * q * P : BLOCK + 2 * (q + 1) * P, :],
+                    in_=passed_of[u][q][:].rearrange("p e n t -> p (e n) t"),
+                )
+
+        def quantise(u):
+            codes = quantised.tile([P, HALF], U32, align_bytes=64)
+            scales = quantised.tile([P, HALF], U8, align_bytes=64)
+            codes_of[u] = (codes, scales)
+            nc.vector.quantize_mx(
+                out=codes[:].bitcast(FP8X4),
+                scales=scales[:],
+                in_=grouped_of[u][:].rearrange("p n t -> p (n t)"),
+            )
+
+        def open_sums(w, c, own_banks):
+            if own_banks:
+                tiles = [
+                    psum.tile([P, B], F32, name="acc", tag="bank%d" % (PACK * (c % 2) + t)) for t in range(PACK)
+                ]
+                accs_of[(w, c)] = [tile[:] for tile in tiles]
+            else:
+                pairs = [
+                    psum.tile([P, 2, B], F32, name="acc_pair", tag="bank%d" % (pair_banks(w, c) + q)) for q in range(2)
+                ]
+                accs_of[(w, c)] = [pairs[t % 2][:, t // 2, :] for t in range(PACK)]
+
+        def one_pass(w, c, g, t, codes, scales, k):
+            cols = slice(k * BLOCK + t * P, k * BLOCK + (t + 1) * P)
+            nc.tensor.matmul_mx(
+                out=accs_of[(w, c)][t],
+                lhsT=codes[:, cols].bitcast(FP8X4),
+                lhsT_scale=scales[:, cols],
+                rhs=moving[w][g][0].bitcast(FP8X4),
+                rhs_scale=moving[w][g][1],
+                start=(g == 0),
+                stop=(g == CHUNKS - 1),
+            )
+
+        def passes(u):
+            codes, scales = codes_of[u]
+            for k, (step, j) in enumerate(units[u]):
+                w, h, g = place_of(step)
+                c = 2 * h + j
+                if shares_banks(w, c):
+                    if g == 0:
+                        open_sums(w, c, False)
+                    held.setdefault((w, c), []).append((codes, scales, k))
+                    for t in range(2):
+                        one_pass(w, c, g, t, codes, scales, k)
+                    if g == CHUNKS - 1:
+                        for t in range(2, PACK):
+                            for gg, (cd, sc, kk) in enumerate(held[(w, c)]):
+                                one_pass(w, c, gg, t, cd, sc, kk)
+                else:
+                    if g == 0:
+                        open_sums(w, c, True)
+                    for t in range(PACK):
+                        one_pass(w, c, g, t, codes, scales, k)
 
         r_of = {}
         rh_grouped_of = {}
@@ -189,7 +307,7 @@ def tile_recurrentffn_pa_kernel(tc, x, hidden_state, W_r, b_r, W_g, b_g, W_up, b
             for t in range(PACK):
                 i = c * PACK + t
                 nc.scalar.activation(
-                    out=r_of[c][:, t, :], in_=accs_of[(0, c)][t][:], func=ACT.Sigmoid, bias=bias_of[0][:, i : i + 1]
+                    out=r_of[c][:, t, :], in_=accs_of[(0, c)][t], func=ACT.Sigmoid, bias=bias_of[0][:, i : i + 1]
                 )
 
         def reset_times_hidden(c):
@@ -212,10 +330,7 @@ def tile_recurrentffn_pa_kernel(tc, x, hidden_state, W_r, b_r, W_g, b_g, W_up, b
             for t in range(PACK):
                 i = c * PACK + t
                 nc.scalar.activation(
-                    out=silu_gate[:, i, :],
-                    in_=accs_of[(1, c)][t][:],
-                    func=ACT.Silu,
-                    bias=bias_of[1][:, i : i + 1],
+                    out=silu_gate[:, i, :], in_=accs_of[(1, c)][t], func=ACT.Silu, bias=bias_of[1][:, i : i + 1]
                 )
 
         def up_product(c):
@@ -224,14 +339,14 @@ def tile_recurrentffn_pa_kernel(tc, x, hidden_state, W_r, b_r, W_g, b_g, W_up, b
                 i = c * PACK + t
                 nc.vector.scalar_tensor_tensor(
                     out=product[:, t, :],
-                    in0=accs_of[(2, c)][t][:],
+                    in0=accs_of[(2, c)][t],
                     scalar=bias_of[2][:, i : i + 1],
                     in1=silu_gate[:, i, :],
                     op0=ALU.add,
                     op1=ALU.mult,
                 )
             for s in range(B_TILES):
-                out_ps_of[(c, s)] = psum.tile([P, BLOCK], F32, name="out_ps", tag=bank_of(c % 2, s))
+                out_ps_of[(c, s)] = psum.tile([P, BLOCK], F32, name="out_ps", tag="bank%d" % (OUT_BANKS[c] + s))
                 for t in range(PACK):
                     nc.tensor.transpose(
                         out_ps_of[(c, s)][:, t * P : (t + 1) * P], product[:, t, s * P : (s + 1) * P], ident_f32[:]
@@ -243,37 +358,46 @@ def tile_recurrentffn_pa_kernel(tc, x, hidden_state, W_r, b_r, W_g, b_g, W_up, b
                 copies[s](out=out_sb[:], in_=out_ps_of[(c, s)][:])
                 nc.sync.dma_start(out=out[s * P : (s + 1) * P, c * BLOCK : (c + 1) * BLOCK], in_=out_sb[:])
 
-        for s in range(STEPS + 2):
-            finish_w, finish_h, finish_g = place_of(s - 2) if s >= 2 else (None, None, None)
-            if finish_g != CHUNKS - 1:
-                finish_w = None
-            first_c = 2 * finish_h if finish_w is not None else None
-            if finish_w == 0:
-                reset_sigmoid(first_c)
-                reset_sigmoid(first_c + 1)
-            if finish_w == 1:
-                gate_silu(first_c)
-                gate_silu(first_c + 1)
-            if finish_w == 2:
-                up_product(first_c)
-                up_product(first_c + 1)
-            if s < STEPS:
-                regroup_piece(nc.vector.tensor_copy, s, 0)
-                regroup_piece(nc.vector.tensor_copy if finish_w == 1 else nc.scalar.copy, s, 1)
-            if 1 <= s <= STEPS:
-                quantise_piece(s - 1, 1)
-            if finish_w == 0:
-                reset_times_hidden(first_c)
-            if s < STEPS:
-                quantise_piece(s, 0)
-            if finish_w == 0:
-                reset_times_hidden(first_c + 1)
-                reset_quantise(first_c)
-                reset_quantise(first_c + 1)
-            if finish_w == 2:
-                last = s == STEPS + 1
-                up_store(first_c, [nc.scalar.copy, nc.scalar.copy])
-                up_store(first_c + 1, [nc.scalar.copy, nc.vector.tensor_copy if last else nc.scalar.copy])
-            if 1 <= s <= STEPS:
-                passes(s - 1)
-            load_step(s + RAW_BUFS)
+        for it in range(STEPS + LQ + 6):
+            act_now = act_part.get(it, [])
+            dve_now = dve_part.get(it, [])
+            if it < STEPS:
+                grouped_of[it] = regroup.tile([P, HALF, PACK], BF16, name="grouped", align_bytes=64)
+                share = SHARE_NORMAL
+                if any(w == 1 for w, c in act_now):
+                    share = SHARE_SILU
+                if it in route_units:
+                    share = SHARE_ROUTE
+                share = SHARES.get(it, share)
+                regroup_cols(nc.vector.tensor_copy, it, 0, share)
+                if it in route_units:
+                    regroup_cols(nc.scalar.copy, it, share, BLOCK)
+                    copy_passed(it)
+                else:
+                    regroup_cols(nc.scalar.copy, it, share, HALF)
+            for w, c in dve_now:
+                if w == 2:
+                    up_product(c)
+                else:
+                    reset_times_hidden(c)
+            u = it - LQ
+            if 0 <= u < STEPS:
+                quantise(u)
+            for w, c in dve_now:
+                if w == 0:
+                    reset_quantise(c)
+            for w, c in act_now:
+                if w == 0:
+                    reset_sigmoid(c)
+                else:
+                    gate_silu(c)
+            for w, c in store_part.get(it, []):
+                last = c == BLOCKS - 1
+                up_store(c, [nc.scalar.copy, nc.vector.tensor_copy if last else nc.scalar.copy])
+            if it == 1:
+                prepare_acts()
+            if it + 1 in route_units:
+                pass_through(it + 1)
+            if 0 <= u < STEPS:
+                passes(u)
+            load_step(it + RAW_BUFS)

@@ -23,6 +23,7 @@ BLOCKS = H // BLOCK
 H_TILES = H // P
 B_TILES = B // P
 RUN = 4
+RUN_IN_ORDER = 8
 WEIGHTS = 3
 HALF = 2 * BLOCK
 HALVES = H // HALF
@@ -201,8 +202,8 @@ def tile_recurrentffn_pa_kernel(tc, x, hidden_state, W_r, b_r, W_g, b_g, W_up, b
             in_order = place_of(step0)[0] != 0
             if in_order and step0 == step1 and lo < hi:
                 copy(
-                    out=grouped_of[u][:, lo:hi, :].rearrange("p (n i) t -> p n t i", i=RUN),
-                    in_=raw_of[step0][:, :, lo:hi].rearrange("p t (n i) -> p n t i", i=RUN),
+                    out=grouped_of[u][:, lo:hi, :].rearrange("p (n i) t -> p n t i", i=RUN_IN_ORDER),
+                    in_=raw_of[step0][:, :, lo:hi].rearrange("p t (n i) -> p n t i", i=RUN_IN_ORDER),
                 )
                 return
             for k, (step, j) in enumerate(units[u]):
@@ -211,13 +212,14 @@ def tile_recurrentffn_pa_kernel(tc, x, hidden_state, W_r, b_r, W_g, b_g, W_up, b
                 if a >= b:
                     continue
                 piece = grouped_of[u][:, k * BLOCK : (k + 1) * BLOCK, :]
+                run = RUN_IN_ORDER if in_order else RUN
                 if in_order:
-                    places = piece[:, a:b, :].rearrange("p (n i) t -> p n t i", i=RUN)
+                    places = piece[:, a:b, :].rearrange("p (n i) t -> p n t i", i=run)
                 else:
                     places = piece.rearrange("p (i n) t -> p n t i", i=RUN)[:, a // RUN : b // RUN, :, :]
                 copy(
                     out=places,
-                    in_=raw_of[step][:, :, j * BLOCK + a : j * BLOCK + b].rearrange("p t (n i) -> p n t i", i=RUN),
+                    in_=raw_of[step][:, :, j * BLOCK + a : j * BLOCK + b].rearrange("p t (n i) -> p n t i", i=run),
                 )
 
         def pass_through(u):

@@ -30,15 +30,27 @@ HALVES = H // HALF
 STEPS = WEIGHTS * HALVES * CHUNKS
 RAW_BUFS = 8
 GROUP_BUFS = 4
-CODE_BUFS = 8
+CODE_BUFS = 10
 LQ = 1
 LAG_FIRST = 1
 LAG_SECOND = 2
 RH_LAG = 1
 STORE_LAG = 1
-SHARES = {1: 640}
+SHARES = {0: 704}
 LAST_BY_BLOCKS = True
-SHARE_NORMAL = 496
+ACTS_FIRST = 1
+ACTS_Q_LAG = 1
+LATE = 1
+EARLY = 1
+ACTS_EVERY = 1
+BIAS_BEHIND = 3
+FIRST_PARTS = 2
+LAST_QUANT_PARTS = 2
+BIAS_AT = 3
+LAST_TWO_QUEUES = True
+SPLIT_STEPS = 1
+PASSES_AN_ITERATION = 16
+SHARE_NORMAL = 512
 SHARE_SILU = 640
 SHARE_ROUTE = 336
 ROUTE_CHUNKS = ()
@@ -76,32 +88,8 @@ def tile_recurrentffn_pa_kernel(tc, x, hidden_state, W_r, b_r, W_g, b_g, W_up, b
         def pair_banks(w, c):
             return PACK + 2 * ((w * HALVES + c // 2) % 2)
 
-        act_part = {}
-        dve_part = {}
-        store_part = {}
-        for u in range(STEPS):
-            for step, j in units[u]:
-                w, h, g = place_of(step)
-                c = 2 * h + j
-                if g == CHUNKS - 1:
-                    at = u + LQ + (LAG_SECOND if shares_banks(w, c) else LAG_FIRST)
-                    if w == 0:
-                        act_part.setdefault(at, []).append((w, c))
-                        dve_part.setdefault(at + RH_LAG, []).append((w, c))
-                    if w == 1:
-                        act_part.setdefault(at, []).append((w, c))
-                    if w == 2:
-                        dve_part.setdefault(at, []).append((w, c))
-                        store_part.setdefault(at + (0 if c == BLOCKS - 1 else STORE_LAG), []).append((w, c))
-
         b_r_sb = const.tile([P, BLOCKS, PACK], BF16)
-        nc.scalar.dma_start(out=b_r_sb[:], in_=b_r.rearrange("(c p t) -> p c t", p=P, t=PACK))
         bias_rows = const.tile([P, P], BF16)
-        for w, b in [(1, b_g), (2, b_up)]:
-            nc.scalar.dma_start(
-                out=bias_rows[(w - 1) * H_TILES : w * H_TILES, :],
-                in_=b.rearrange("(i p) -> i p", p=P),
-            )
         nc.vector.memset(bias_rows[2 * H_TILES : 4 * H_TILES, :], 0.0)
         nc.vector.memset(bias_rows[4 * H_TILES : P, :], 0.0)
 
@@ -123,19 +111,31 @@ def tile_recurrentffn_pa_kernel(tc, x, hidden_state, W_r, b_r, W_g, b_g, W_up, b
 
         acts_sb = const.tile([P, B_TILES, C], BF16)
 
-        def load_acts():
-            nc.sync.dma_start(out=acts_sb[:, :, 0:D], in_=x.rearrange("(s p) d -> p s d", p=P))
-            for k0 in range(D, C, H // 2):
+        def load_acts(g):
+            source = x if g == 0 else hidden_state[:, (g - 1) * K_PASS : g * K_PASS]
+            nc.sync.dma_start(
+                out=acts_sb[:, :, g * K_PASS : (g + 1) * K_PASS], in_=source.rearrange("(s p) d -> p s d", p=P)
+            )
+
+        def load_biases():
+            nc.sync.dma_start(out=b_r_sb[:], in_=b_r.rearrange("(c p t) -> p c t", p=P, t=PACK))
+            for w, b in [(1, b_g), (2, b_up)]:
                 nc.sync.dma_start(
-                    out=acts_sb[:, :, k0 : k0 + H // 2],
-                    in_=hidden_state[:, k0 - D : k0 - D + H // 2].rearrange("(s p) d -> p s d", p=P),
+                    out=bias_rows[(w - 1) * H_TILES : w * H_TILES, :],
+                    in_=b.rearrange("(i p) -> i p", p=P),
                 )
 
-        load_step(0, 2)
-        load_step(1)
-        load_acts()
-        for s in range(2, RAW_BUFS):
-            load_step(s)
+        acts_behind = {ACTS_FIRST + ACTS_EVERY * g: g for g in range(CHUNKS)}
+
+        def load_next(s):
+            load_step(s, FIRST_PARTS if s < SPLIT_STEPS else 1)
+            if s in acts_behind:
+                load_acts(acts_behind[s])
+            if s == BIAS_BEHIND:
+                load_biases()
+
+        for s in range(RAW_BUFS):
+            load_next(s)
 
         ident_bf = const.tile([P, P], BF16)
         make_identity(nc, ident_bf[:])
@@ -153,32 +153,43 @@ def tile_recurrentffn_pa_kernel(tc, x, hidden_state, W_r, b_r, W_g, b_g, W_up, b
         acts_codes = const.tile([P, CHUNKS, B], U32, align_bytes=64)
         acts_scales = const.tile([P, CHUNKS, B], U8, align_bytes=64)
 
-        def prepare_acts():
-            for g in range(CHUNKS):
-                acts_ps = psum.tile([P, 2, B], F32, tag="bank%d" % g)
-                for u in range(2):
-                    for s in range(B_TILES):
-                        words = acts_sb[:, s, g * K_PASS : (g + 1) * K_PASS].bitcast(F32)
-                        nc.tensor.transpose(
-                            acts_ps[:, u, s * P : (s + 1) * P],
-                            words.rearrange("p (j u) -> p j u", u=2)[:, :, u],
-                            ident_f32[:],
-                        )
-                nc.scalar.copy(
-                    out=acts_grouped[:, g, :, :]
-                    .rearrange("p b t -> p (b t)")
-                    .bitcast(F32)
-                    .rearrange("p (b u) -> p b u", u=2),
-                    in_=acts_ps[:].rearrange("p u b -> p b u"),
-                )
-                nc.vector.quantize_mx(
-                    out=acts_codes[:, g, :].bitcast(FP8X4),
-                    scales=acts_scales[:, g, :],
-                    in_=acts_grouped[:, g, :, :].rearrange("p b t -> p (b t)"),
-                )
-            bias_ps = psum.tile([P, P], BF16, tag="bank%d" % CHUNKS)
-            nc.tensor.transpose(bias_ps[:], bias_rows[:], ident_bf[:])
-            nc.vector.tensor_copy(out=bias[:], in_=bias_ps[:])
+        acts_ps_of = {}
+
+        def transpose_acts(g):
+            acts_ps_of[g] = psum.tile([P, 2, B], F32, name="acts_ps", tag="bank%d" % (6 + g % 2))
+            for u in range(2):
+                for s in range(B_TILES):
+                    words = acts_sb[:, s, g * K_PASS : (g + 1) * K_PASS].bitcast(F32)
+                    nc.tensor.transpose(
+                        acts_ps_of[g][:, u, s * P : (s + 1) * P],
+                        words.rearrange("p (j u) -> p j u", u=2)[:, :, u],
+                        ident_f32[:],
+                    )
+
+        def copy_acts(g):
+            nc.scalar.copy(
+                out=acts_grouped[:, g, :, :]
+                .rearrange("p b t -> p (b t)")
+                .bitcast(F32)
+                .rearrange("p (b u) -> p b u", u=2),
+                in_=acts_ps_of[g][:].rearrange("p u b -> p b u"),
+            )
+
+        def quantise_acts(g):
+            nc.vector.quantize_mx(
+                out=acts_codes[:, g, :].bitcast(FP8X4),
+                scales=acts_scales[:, g, :],
+                in_=acts_grouped[:, g, :, :].rearrange("p b t -> p (b t)"),
+            )
+
+        bias_ps_of = {}
+
+        def transpose_biases():
+            bias_ps_of[0] = psum.tile([P, P], BF16, name="bias_ps", tag="bank7")
+            nc.tensor.transpose(bias_ps_of[0][:], bias_rows[:], ident_bf[:])
+
+        def copy_biases():
+            nc.vector.tensor_copy(out=bias[:], in_=bias_ps_of[0][:])
             nc.vector.tensor_copy(
                 out=bias[:, 2 * H_TILES : 3 * H_TILES], in_=b_r_sb[:].rearrange("p c t -> p (c t)")
             )
@@ -249,11 +260,14 @@ def tile_recurrentffn_pa_kernel(tc, x, hidden_state, W_r, b_r, W_g, b_g, W_up, b
             codes = quantised.tile([P, HALF], U32, align_bytes=64)
             scales = quantised.tile([P, HALF], U8, align_bytes=64)
             codes_of[u] = (codes, scales)
-            nc.vector.quantize_mx(
-                out=codes[:].bitcast(FP8X4),
-                scales=scales[:],
-                in_=grouped_of[u][:].rearrange("p n t -> p (n t)"),
-            )
+            parts = LAST_QUANT_PARTS if u == STEPS - 1 else 1
+            width = HALF // parts
+            for k in range(parts):
+                nc.vector.quantize_mx(
+                    out=codes[:, k * width : (k + 1) * width].bitcast(FP8X4),
+                    scales=scales[:, k * width : (k + 1) * width],
+                    in_=grouped_of[u][:, k * width : (k + 1) * width, :].rearrange("p n t -> p (n t)"),
+                )
 
         def open_sums(w, c, own_banks):
             if own_banks:
@@ -280,6 +294,7 @@ def tile_recurrentffn_pa_kernel(tc, x, hidden_state, W_r, b_r, W_g, b_g, W_up, b
             )
 
         def passes(u):
+            closed = []
             codes, scales = codes_of[u]
             for k, (step, j) in enumerate(units[u]):
                 w, h, g = place_of(step)
@@ -299,6 +314,9 @@ def tile_recurrentffn_pa_kernel(tc, x, hidden_state, W_r, b_r, W_g, b_g, W_up, b
                         open_sums(w, c, True)
                     for t in range(PACK):
                         one_pass(w, c, g, t, codes, scales, k)
+                if g == CHUNKS - 1:
+                    closed.append((w, c))
+            return closed
 
         r_of = {}
         rh_grouped_of = {}
@@ -335,8 +353,11 @@ def tile_recurrentffn_pa_kernel(tc, x, hidden_state, W_r, b_r, W_g, b_g, W_up, b
                     out=silu_gate[:, i, :], in_=accs_of[(1, c)][t], func=ACT.Silu, bias=bias_of[1][:, i : i + 1]
                 )
 
+        product_of = {}
+
         def up_product(c):
             product = work.tile([P, PACK, B], F32, tag="four_tiles")
+            product_of[c] = product
             for t in range(PACK):
                 i = c * PACK + t
                 nc.vector.scalar_tensor_tensor(
@@ -347,6 +368,9 @@ def tile_recurrentffn_pa_kernel(tc, x, hidden_state, W_r, b_r, W_g, b_g, W_up, b
                     op0=ALU.add,
                     op1=ALU.mult,
                 )
+
+        def up_transpose(c):
+            product = product_of[c]
             for s in range(B_TILES):
                 out_ps_of[(c, s)] = psum.tile([P, BLOCK], F32, name="out_ps", tag="bank%d" % (OUT_BANKS[c] + s))
                 for t in range(PACK):
@@ -358,9 +382,36 @@ def tile_recurrentffn_pa_kernel(tc, x, hidden_state, W_r, b_r, W_g, b_g, W_up, b
             for s in range(B_TILES):
                 out_sb = stores.tile([P, BLOCK], F32)
                 copies[s](out=out_sb[:], in_=out_ps_of[(c, s)][:])
-                nc.sync.dma_start(out=out[s * P : (s + 1) * P, c * BLOCK : (c + 1) * BLOCK], in_=out_sb[:])
+                queue = nc.scalar if (c == BLOCKS - 1 and s == 0 and LAST_TWO_QUEUES) else nc.sync
+                queue.dma_start(out=out[s * P : (s + 1) * P, c * BLOCK : (c + 1) * BLOCK], in_=out_sb[:])
 
-        for it in range(STEPS + LQ + 6):
+        act_part = {}
+        dve_part = {}
+        store_part = {}
+        waiting = []
+        moving_ready = []
+        owner = {}
+
+        def banks_of(w, c):
+            if shares_banks(w, c):
+                return [pair_banks(w, c), pair_banks(w, c) + 1]
+            return [PACK * (c % 2) + t for t in range(PACK)]
+
+        def may_go(u):
+            for step, j in units[u]:
+                w, h, g = place_of(step)
+                if (w == 0 or g == 0, g) not in moving_ready:
+                    return False
+                if g == 0 and any(bank in owner for bank in banks_of(w, 2 * h + j)):
+                    return False
+            return True
+
+        def leave(w, c, banks):
+            for bank in banks:
+                if owner.get(bank) == (w, c):
+                    owner.pop(bank)
+
+        for it in range(STEPS + 12):
             act_now = act_part.get(it, [])
             dve_now = dve_part.get(it, [])
             if it < STEPS:
@@ -378,28 +429,69 @@ def tile_recurrentffn_pa_kernel(tc, x, hidden_state, W_r, b_r, W_g, b_g, W_up, b
                 else:
                     regroup_cols(nc.scalar.copy, it, share, HALF)
             for w, c in dve_now:
-                if w == 2:
-                    up_product(c)
-                else:
+                if w == 0:
                     reset_times_hidden(c)
-            u = it - LQ
-            if 0 <= u < STEPS:
-                quantise(u)
+            for u in [it - LQ, it]:
+                if 0 <= u < STEPS and (u < EARLY or u >= STEPS - LATE) == (u == it):
+                    quantise(u)
+                    waiting.append(u)
             for w, c in dve_now:
                 if w == 0:
                     reset_quantise(c)
+                    moving_ready.append((False, c + 1))
+                else:
+                    up_product(c)
+                    leave(w, c, [bank for bank in banks_of(w, c) if bank not in (OUT_BANKS[c], OUT_BANKS[c] + 1)])
+                    owner[OUT_BANKS[c]] = (w, c)
+                    owner[OUT_BANKS[c] + 1] = (w, c)
             for w, c in act_now:
                 if w == 0:
                     reset_sigmoid(c)
                 else:
                     gate_silu(c)
+                leave(w, c, banks_of(w, c))
             for w, c in store_part.get(it, []):
-                last = c == BLOCKS - 1
-                up_store(c, [nc.scalar.copy, nc.vector.tensor_copy if last else nc.scalar.copy])
-            if it == 1:
-                prepare_acts()
+                if c != BLOCKS - 1:
+                    up_store(c, [nc.scalar.copy, nc.scalar.copy])
+                    leave(w, c, [OUT_BANKS[c], OUT_BANKS[c] + 1])
+            for g in range(CHUNKS):
+                if it == ACTS_FIRST + ACTS_EVERY * g + 1 + ACTS_Q_LAG:
+                    quantise_acts(g)
+                    moving_ready.append((True, g))
+                if it == ACTS_FIRST + ACTS_EVERY * g + 1:
+                    copy_acts(g)
+            if it == BIAS_AT + 1:
+                copy_biases()
             if it + 1 in route_units:
                 pass_through(it + 1)
-            if 0 <= u < STEPS:
-                passes(u)
-            load_step(it + RAW_BUFS)
+            queued = 0
+            while len(waiting) > 0 and may_go(waiting[0]):
+                u = waiting.pop(0)
+                for step, j in units[u]:
+                    w, h, g = place_of(step)
+                    for bank in banks_of(w, 2 * h + j):
+                        owner[bank] = (w, 2 * h + j)
+                closed = passes(u)
+                queued += 2 * PACK
+                for w, c in closed:
+                    at = it + (LAG_SECOND if shares_banks(w, c) else LAG_FIRST) + queued // PASSES_AN_ITERATION
+                    if w == 0:
+                        act_part.setdefault(at, []).append((w, c))
+                        dve_part.setdefault(at + RH_LAG, []).append((w, c))
+                    if w == 1:
+                        act_part.setdefault(at, []).append((w, c))
+                    if w == 2:
+                        dve_part.setdefault(at, []).append((w, c))
+                        store_part.setdefault(at + (0 if c == BLOCKS - 1 else STORE_LAG), []).append((w, c))
+            for w, c in dve_now:
+                if w == 2:
+                    up_transpose(c)
+                    if c == BLOCKS - 1:
+                        up_store(c, [nc.scalar.copy, nc.vector.tensor_copy])
+            for g in range(CHUNKS):
+                if it == ACTS_FIRST + ACTS_EVERY * g:
+                    transpose_acts(g)
+            if it == BIAS_AT:
+                transpose_biases()
+            if it + RAW_BUFS < STEPS:
+                load_next(it + RAW_BUFS)

@@ -109,18 +109,18 @@ def tile_recurrentffn_pa_kernel(tc, x, hidden_state, W_r, b_r, W_g, b_g, W_up, b
                     ].rearrange("(p t) n -> p t n", t=PACK),
                 )
 
-        acts_sb = const.tile([P, B_TILES, C], BF16)
+        acts_sb = [const.tile([P, B_TILES, K_PASS], BF16, name="acts_sb%d" % g) for g in range(CHUNKS)]
 
         def load_acts(g):
             source = x if g == 0 else hidden_state[:, (g - 1) * K_PASS : g * K_PASS]
             nc.sync.dma_start(
-                out=acts_sb[:, :, g * K_PASS : (g + 1) * K_PASS], in_=source.rearrange("(s p) d -> p s d", p=P)
+                out=acts_sb[g][:], in_=source.rearrange("(s p) d -> p s d", p=P)
             )
 
         def load_biases():
-            nc.sync.dma_start(out=b_r_sb[:], in_=b_r.rearrange("(c p t) -> p c t", p=P, t=PACK))
+            nc.scalar.dma_start(out=b_r_sb[:], in_=b_r.rearrange("(c p t) -> p c t", p=P, t=PACK))
             for w, b in [(1, b_g), (2, b_up)]:
-                nc.sync.dma_start(
+                nc.scalar.dma_start(
                     out=bias_rows[(w - 1) * H_TILES : w * H_TILES, :],
                     in_=b.rearrange("(i p) -> i p", p=P),
                 )
@@ -131,9 +131,8 @@ def tile_recurrentffn_pa_kernel(tc, x, hidden_state, W_r, b_r, W_g, b_g, W_up, b
             load_step(s, FIRST_PARTS if s < SPLIT_STEPS else 1)
             if s in acts_behind:
                 load_acts(acts_behind[s])
-            if s == BIAS_BEHIND:
-                load_biases()
 
+        load_biases()
         for s in range(RAW_BUFS):
             load_next(s)
 
@@ -159,7 +158,7 @@ def tile_recurrentffn_pa_kernel(tc, x, hidden_state, W_r, b_r, W_g, b_g, W_up, b
             acts_ps_of[g] = psum.tile([P, 2, B], F32, name="acts_ps", tag="bank%d" % (6 + g % 2))
             for u in range(2):
                 for s in range(B_TILES):
-                    words = acts_sb[:, s, g * K_PASS : (g + 1) * K_PASS].bitcast(F32)
+                    words = acts_sb[g][:, s, :].bitcast(F32)
                     nc.tensor.transpose(
                         acts_ps_of[g][:, u, s * P : (s + 1) * P],
                         words.rearrange("p (j u) -> p j u", u=2)[:, :, u],

@@ -38,20 +38,22 @@ RH_LAG = 1
 STORE_LAG = 1
 SHARES = {0: 704}
 LAST_BY_BLOCKS = True
+ACTS_BEHIND = [1, 2, 3, 4, 5]
 ACTS_FIRST = 1
 ACTS_Q_LAG = 1
 LATE = 1
 EARLY = 1
 ACTS_EVERY = 1
-BIAS_BEHIND = 3
+BIAS_BEHIND = 5
 FIRST_PARTS = 2
 LAST_QUANT_PARTS = 2
-BIAS_AT = 3
+BIAS_AT = 6
 LAST_TWO_QUEUES = True
-SPLIT_STEPS = 1
+SPLIT_STEPS = 0
 PASSES_AN_ITERATION = 16
-SHARE_NORMAL = 512
-SHARE_SILU = 640
+SHARE_NORMAL = 480
+SHARE_W_R = 512
+SHARE_SILU = 608
 SHARE_ROUTE = 336
 ROUTE_CHUNKS = ()
 
@@ -118,21 +120,22 @@ def tile_recurrentffn_pa_kernel(tc, x, hidden_state, W_r, b_r, W_g, b_g, W_up, b
             )
 
         def load_biases():
-            nc.scalar.dma_start(out=b_r_sb[:], in_=b_r.rearrange("(c p t) -> p c t", p=P, t=PACK))
+            nc.sync.dma_start(out=b_r_sb[:], in_=b_r.rearrange("(c p t) -> p c t", p=P, t=PACK))
             for w, b in [(1, b_g), (2, b_up)]:
-                nc.scalar.dma_start(
+                nc.sync.dma_start(
                     out=bias_rows[(w - 1) * H_TILES : w * H_TILES, :],
                     in_=b.rearrange("(i p) -> i p", p=P),
                 )
 
-        acts_behind = {ACTS_FIRST + ACTS_EVERY * g: g for g in range(CHUNKS)}
+        acts_behind = {ACTS_BEHIND[g]: g for g in range(CHUNKS)}
 
         def load_next(s):
             load_step(s, FIRST_PARTS if s < SPLIT_STEPS else 1)
             if s in acts_behind:
                 load_acts(acts_behind[s])
+            if s == BIAS_BEHIND:
+                load_biases()
 
-        load_biases()
         for s in range(RAW_BUFS):
             load_next(s)
 
@@ -415,7 +418,7 @@ def tile_recurrentffn_pa_kernel(tc, x, hidden_state, W_r, b_r, W_g, b_g, W_up, b
             dve_now = dve_part.get(it, [])
             if it < STEPS:
                 grouped_of[it] = regroup.tile([P, HALF, PACK], BF16, name="grouped", align_bytes=64)
-                share = SHARE_NORMAL
+                share = SHARE_W_R if it < HALVES * CHUNKS else SHARE_NORMAL
                 if any(w == 1 for w, c in act_now):
                     share = SHARE_SILU
                 if it in route_units:
@@ -430,10 +433,10 @@ def tile_recurrentffn_pa_kernel(tc, x, hidden_state, W_r, b_r, W_g, b_g, W_up, b
             for w, c in dve_now:
                 if w == 0:
                     reset_times_hidden(c)
-            for u in [it - LQ, it]:
-                if 0 <= u < STEPS and (u < EARLY or u >= STEPS - LATE) == (u == it):
-                    quantise(u)
-                    waiting.append(u)
+            behind = 0 if (it < EARLY or it >= STEPS - LATE) else LQ
+            while len(codes_of) < STEPS and len(codes_of) <= it - behind:
+                waiting.append(len(codes_of))
+                quantise(len(codes_of))
             for w, c in dve_now:
                 if w == 0:
                     reset_quantise(c)
@@ -454,10 +457,10 @@ def tile_recurrentffn_pa_kernel(tc, x, hidden_state, W_r, b_r, W_g, b_g, W_up, b
                     up_store(c, [nc.scalar.copy, nc.scalar.copy])
                     leave(w, c, [OUT_BANKS[c], OUT_BANKS[c] + 1])
             for g in range(CHUNKS):
-                if it == ACTS_FIRST + ACTS_EVERY * g + 1 + ACTS_Q_LAG:
+                if it == ACTS_BEHIND[g] + 1 + ACTS_Q_LAG:
                     quantise_acts(g)
                     moving_ready.append((True, g))
-                if it == ACTS_FIRST + ACTS_EVERY * g + 1:
+                if it == ACTS_BEHIND[g] + 1:
                     copy_acts(g)
             if it == BIAS_AT + 1:
                 copy_biases()
@@ -488,7 +491,7 @@ def tile_recurrentffn_pa_kernel(tc, x, hidden_state, W_r, b_r, W_g, b_g, W_up, b
                     if c == BLOCKS - 1:
                         up_store(c, [nc.scalar.copy, nc.vector.tensor_copy])
             for g in range(CHUNKS):
-                if it == ACTS_FIRST + ACTS_EVERY * g:
+                if it == ACTS_BEHIND[g]:
                     transpose_acts(g)
             if it == BIAS_AT:
                 transpose_biases()

@@ -51,7 +51,7 @@ BIAS_AT = 6
 LAST_TWO_QUEUES = True
 SPLIT_STEPS = 0
 PASSES_AN_ITERATION = 16
-SHARE_NORMAL = 480
+SHARE_NORMAL = 496
 SHARE_W_R = 512
 SHARE_SILU = 608
 SHARE_ROUTE = 336

@@ -228,12 +228,18 @@ def tile_recurrentffn_pa_kernel(tc, x, hidden_state, W_r, b_r, W_g, b_g, W_up, b
                 run = RUN_IN_ORDER if in_order else RUN
                 if in_order:
                     places = piece[:, a:b, :].rearrange("p (n i) t -> p n t i", i=run)
+                    copy(
+                        out=places,
+                        in_=raw_of[step][:, :, j * BLOCK + a : j * BLOCK + b].rearrange("p t (n i) -> p n t i", i=run),
+                    )
                 else:
-                    places = piece.rearrange("p (i n) t -> p n t i", i=RUN)[:, a // RUN : b // RUN, :, :]
-                copy(
-                    out=places,
-                    in_=raw_of[step][:, :, j * BLOCK + a : j * BLOCK + b].rearrange("p t (n i) -> p n t i", i=run),
-                )
+                    places = piece.rearrange("p (i n e) t -> p n t e i", i=RUN, e=2)[:, a // (2 * RUN) : b // (2 * RUN), :, :, :]
+                    copy(
+                        out=places,
+                        in_=raw_of[step][:, :, j * BLOCK + a : j * BLOCK + b].rearrange(
+                            "p t (n e i) -> p n t e i", e=2, i=RUN
+                        ),
+                    )
 
         def pass_through(u):
             step, j = units[u][1]

from contextlib import ExitStack

import concourse.mybir as mybir
from concourse.masks import make_identity

FP8X4 = mybir.dt.float8_e4m3fn_x4
BF16 = mybir.dt.bfloat16
F32 = mybir.dt.float32
U32 = mybir.dt.uint32
U8 = mybir.dt.uint8
ACT = mybir.ActivationFunctionType
ALU = mybir.AluOpType

P = 128
PACK = 4
K_PASS = P * PACK

B, D, H = 256, 512, 2048
C = D + H
CHUNKS = C // K_PASS
BLOCK = PACK * P
BLOCKS = H // BLOCK
H_TILES = H // P
B_TILES = B // P
RUN = 4
RUN_IN_ORDER = 8
WEIGHTS = 3
HALF = 2 * BLOCK
HALVES = H // HALF
STEPS = WEIGHTS * HALVES * CHUNKS
RAW_BUFS = 8
GROUP_BUFS = 4
CODE_BUFS = 10
LQ = 1
LAG_FIRST = 1
LAG_SECOND = 2
RH_LAG = 1
STORE_LAG = 1
SHARES = {0: 704}
LAST_BY_BLOCKS = True
ACTS_BEHIND = [1, 2, 3, 4, 5]
ACTS_FIRST = 1
ACTS_Q_LAG = 1
LATE = 1
EARLY = 1
ACTS_EVERY = 1
BIAS_BEHIND = 5
FIRST_PARTS = 2
LAST_QUANT_PARTS = 2
BIAS_AT = 6
LAST_TWO_QUEUES = True
SPLIT_STEPS = 0
PASSES_AN_ITERATION = 16
SHARE_NORMAL = 496
SHARE_W_R = 512
SHARE_SILU = 608
SHARE_ROUTE = 336
ROUTE_CHUNKS = ()

OUT_BANKS = [6, 4, 0, 4]
FLOPS = 2 * B * C * H * 3


def tile_recurrentffn_pa_kernel(tc, x, hidden_state, W_r, b_r, W_g, b_g, W_up, b_up, out):
    nc = tc.nc
    weights = [W_r, W_g, W_up]
    with ExitStack() as ctx:
        const = ctx.enter_context(tc.tile_pool(name="const", bufs=1))
        staging = ctx.enter_context(tc.tile_pool(name="staging", bufs=RAW_BUFS))
        regroup = ctx.enter_context(tc.tile_pool(name="regroup", bufs=GROUP_BUFS))
        quantised = ctx.enter_context(tc.tile_pool(name="quantised", bufs=CODE_BUFS))
        work = ctx.enter_context(tc.tile_pool(name="work", bufs=2))
        stores = ctx.enter_context(tc.tile_pool(name="stores", bufs=4))
        psum = ctx.enter_context(tc.psum_pool(name="psum", bufs=1))
        ctx.enter_context(tc.manual_schedule())

        def place_of(s):
            return s // (HALVES * CHUNKS), (s // CHUNKS) % HALVES, s % CHUNKS

        units = [[(s, 0), (s, 1)] for s in range(STEPS)]
        if LAST_BY_BLOCKS:
            last_half = [(STEPS - CHUNKS + g, j) for j in range(2) for g in range(CHUNKS)]
            for k in range(CHUNKS):
                units[STEPS - CHUNKS + k] = last_half[2 * k : 2 * k + 2]
        route_units = [u for u in range(1, STEPS - CHUNKS) if u % CHUNKS in ROUTE_CHUNKS]

        def shares_banks(w, c):
            return c % 2 == 1 and (w, c) != (WEIGHTS - 1, BLOCKS - 1)

        def pair_banks(w, c):
            return PACK + 2 * ((w * HALVES + c // 2) % 2)

        b_r_sb = const.tile([P, BLOCKS, PACK], BF16)
        bias_rows = const.tile([P, P], BF16)
        nc.vector.memset(bias_rows[2 * H_TILES : 4 * H_TILES, :], 0.0)
        nc.vector.memset(bias_rows[4 * H_TILES : P, :], 0.0)

        raw_of = {}

        def load_step(s, parts=1):
            if s >= STEPS:
                return
            w, h, g = place_of(s)
            raw_of[s] = staging.tile([P, PACK, HALF], BF16, name="raw")
            width = HALF // parts
            for k in range(parts):
                nc.sync.dma_start(
                    out=raw_of[s][:, :, k * width : (k + 1) * width],
                    in_=weights[w][
                        g * K_PASS : (g + 1) * K_PASS, h * HALF + k * width : h * HALF + (k + 1) * width
                    ].rearrange("(p t) n -> p t n", t=PACK),
                )

        acts_sb = [const.tile([P, B_TILES, K_PASS], BF16, name="acts_sb%d" % g) for g in range(CHUNKS)]

        def load_acts(g):
            source = x if g == 0 else hidden_state[:, (g - 1) * K_PASS : g * K_PASS]
            nc.sync.dma_start(
                out=acts_sb[g][:], in_=source.rearrange("(s p) d -> p s d", p=P)
            )

        def load_biases():
            nc.sync.dma_start(out=b_r_sb[:], in_=b_r.rearrange("(c p t) -> p c t", p=P, t=PACK))
            for w, b in [(1, b_g), (2, b_up)]:
                nc.sync.dma_start(
                    out=bias_rows[(w - 1) * H_TILES : w * H_TILES, :],
                    in_=b.rearrange("(i p) -> i p", p=P),
                )

        acts_behind = {ACTS_BEHIND[g]: g for g in range(CHUNKS)}

        def load_next(s):
            load_step(s, FIRST_PARTS if s < SPLIT_STEPS else 1)
            if s in acts_behind:
                load_acts(acts_behind[s])
            if s == BIAS_BEHIND:
                load_biases()

        for s in range(RAW_BUFS):
            load_next(s)

        ident_bf = const.tile([P, P], BF16)
        make_identity(nc, ident_bf[:])
        ident_f32 = const.tile([P, P], F32)
        make_identity(nc, ident_f32[:])

        zero = const.tile([P, 1], F32)
        nc.vector.memset(zero[:], 0.0)
        half_one = const.tile([P, 1], F32)
        nc.scalar.activation(out=half_one[:], in_=zero[:], func=ACT.Sigmoid)

        bias = const.tile([P, P], F32)
        bias_of = [bias[:, 2 * H_TILES : 3 * H_TILES], bias[:, 0:H_TILES], bias[:, H_TILES : 2 * H_TILES]]
        acts_grouped = const.tile([P, CHUNKS, B, PACK], BF16, align_bytes=64)
        acts_codes = const.tile([P, CHUNKS, B], U32, align_bytes=64)
        acts_scales = const.tile([P, CHUNKS, B], U8, align_bytes=64)

        acts_ps_of = {}

        def transpose_acts(g):
            acts_ps_of[g] = psum.tile([P, 2, B], F32, name="acts_ps", tag="bank%d" % (6 + g % 2))
            for u in range(2):
                for s in range(B_TILES):
                    words = acts_sb[g][:, s, :].bitcast(F32)
                    nc.tensor.transpose(
                        acts_ps_of[g][:, u, s * P : (s + 1) * P],
                        words.rearrange("p (j u) -> p j u", u=2)[:, :, u],
                        ident_f32[:],
                    )

        def copy_acts(g):
            nc.scalar.copy(
                out=acts_grouped[:, g, :, :]
                .rearrange("p b t -> p (b t)")
                .bitcast(F32)
                .rearrange("p (b u) -> p b u", u=2),
                in_=acts_ps_of[g][:].rearrange("p u b -> p b u"),
            )

        def quantise_acts(g):
            nc.vector.quantize_mx(
                out=acts_codes[:, g, :].bitcast(FP8X4),
                scales=acts_scales[:, g, :],
                in_=acts_grouped[:, g, :, :].rearrange("p b t -> p (b t)"),
            )

        bias_ps_of = {}

        def transpose_biases():
            bias_ps_of[0] = psum.tile([P, P], BF16, name="bias_ps", tag="bank7")
            nc.tensor.transpose(bias_ps_of[0][:], bias_rows[:], ident_bf[:])

        def copy_biases():
            nc.vector.tensor_copy(out=bias[:], in_=bias_ps_of[0][:])
            nc.vector.tensor_copy(
                out=bias[:, 2 * H_TILES : 3 * H_TILES], in_=b_r_sb[:].rearrange("p c t -> p (c t)")
            )

        rh_codes = const.tile([P, BLOCKS, B], U32, align_bytes=64)
        rh_scales = const.tile([P, BLOCKS, B], U8, align_bytes=64)
        silu_gate = const.tile([P, H_TILES, B], F32)

        x_and_h = [(acts_codes[:, g, :], acts_scales[:, g, :]) for g in range(CHUNKS)]
        x_and_rh = x_and_h[0:1] + [(rh_codes[:, c, :], rh_scales[:, c, :]) for c in range(BLOCKS)]
        moving = [x_and_h, x_and_rh, x_and_rh]

        grouped_of = {}
        codes_of = {}
        accs_of = {}
        held = {}
        passed_of = {}

        def regroup_cols(copy, u, lo, hi):
            (step0, j0), (step1, j1) = units[u]
            in_order = place_of(step0)[0] != 0
            if in_order and step0 == step1 and lo < hi:
                copy(
                    out=grouped_of[u][:, lo:hi, :].rearrange("p (n i) t -> p n t i", i=RUN_IN_ORDER),
                    in_=raw_of[step0][:, :, lo:hi].rearrange("p t (n i) -> p n t i", i=RUN_IN_ORDER),
                )
                return
            for k, (step, j) in enumerate(units[u]):
                a = max(lo, k * BLOCK) - k * BLOCK
                b = min(hi, (k + 1) * BLOCK) - k * BLOCK
                if a >= b:
                    continue
                piece = grouped_of[u][:, k * BLOCK : (k + 1) * BLOCK, :]
                run = RUN_IN_ORDER if in_order else RUN
                if in_order:
                    places = piece[:, a:b, :].rearrange("p (n i) t -> p n t i", i=run)
                    copy(
                        out=places,
                        in_=raw_of[step][:, :, j * BLOCK + a : j * BLOCK + b].rearrange("p t (n i) -> p n t i", i=run),
                    )
                else:
                    places = piece.rearrange("p (i n e) t -> p n t e i", i=RUN, e=2)[:, a // (2 * RUN) : b // (2 * RUN), :, :, :]
                    copy(
                        out=places,
                        in_=raw_of[step][:, :, j * BLOCK + a : j * BLOCK + b].rearrange(
                            "p t (n e i) -> p n t e i", e=2, i=RUN
                        ),
                    )

        def pass_through(u):
            step, j = units[u][1]
            in_order = place_of(step)[0] != 0
            cols = raw_of[step][:, :, j * BLOCK : (j + 1) * BLOCK]
            view = cols.rearrange("p t (i n) -> p i n t" if in_order else "p t (n i) -> p i n t", i=PACK)
            passed_of[u] = []
            w, h, g = place_of(step)
            free_pair = pair_banks(w, 2 * h + j) if g == 0 else PACK + 2 - (pair_banks(w, 2 * h + j) - PACK)
            for q in range(2):
                passed = psum.tile([P, 2, P, PACK], BF16, name="passed", tag="bank%d" % (free_pair + q))
                passed_of[u].append(passed)
                for e in range(2):
                    nc.tensor.matmul(
                        out=passed[:, e, :, :], lhsT=ident_bf[:], rhs=view[:, 2 * q + e, :, :], start=True, stop=True
                    )

        def copy_passed(u):
            for q in range(2):
                nc.scalar.copy(
                    out=grouped_of[u][:, BLOCK + 2 * q * P : BLOCK + 2 * (q + 1) * P, :],
                    in_=passed_of[u][q][:].rearrange("p e n t -> p (e n) t"),
                )

        def quantise(u):
            codes = quantised.tile([P, HALF], U32, align_bytes=64)
            scales = quantised.tile([P, HALF], U8, align_bytes=64)
            codes_of[u] = (codes, scales)
            parts = LAST_QUANT_PARTS if u == STEPS - 1 else 1
            width = HALF // parts
            for k in range(parts):
                nc.vector.quantize_mx(
                    out=codes[:, k * width : (k + 1) * width].bitcast(FP8X4),
                    scales=scales[:, k * width : (k + 1) * width],
                    in_=grouped_of[u][:, k * width : (k + 1) * width, :].rearrange("p n t -> p (n t)"),
                )

        def open_sums(w, c, own_banks):
            if own_banks:
                tiles = [
                    psum.tile([P, B], F32, name="acc", tag="bank%d" % (PACK * (c % 2) + t)) for t in range(PACK)
                ]
                accs_of[(w, c)] = [tile[:] for tile in tiles]
            else:
                pairs = [
                    psum.tile([P, 2, B], F32, name="acc_pair", tag="bank%d" % (pair_banks(w, c) + q)) for q in range(2)
                ]
                accs_of[(w, c)] = [pairs[t % 2][:, t // 2, :] for t in range(PACK)]

        def one_pass(w, c, g, t, codes, scales, k):
            cols = slice(k * BLOCK + t * P, k * BLOCK + (t + 1) * P)
            nc.tensor.matmul_mx(
                out=accs_of[(w, c)][t],
                lhsT=codes[:, cols].bitcast(FP8X4),
                lhsT_scale=scales[:, cols],
                rhs=moving[w][g][0].bitcast(FP8X4),
                rhs_scale=moving[w][g][1],
                start=(g == 0),
                stop=(g == CHUNKS - 1),
            )

        def passes(u):
            closed = []
            codes, scales = codes_of[u]
            for k, (step, j) in enumerate(units[u]):
                w, h, g = place_of(step)
                c = 2 * h + j
                if shares_banks(w, c):
                    if g == 0:
                        open_sums(w, c, False)
                    held.setdefault((w, c), []).append((codes, scales, k))
                    for t in range(2):
                        one_pass(w, c, g, t, codes, scales, k)
                    if g == CHUNKS - 1:
                        for t in range(2, PACK):
                            for gg, (cd, sc, kk) in enumerate(held[(w, c)]):
                                one_pass(w, c, gg, t, cd, sc, kk)
                else:
                    if g == 0:
                        open_sums(w, c, True)
                    for t in range(PACK):
                        one_pass(w, c, g, t, codes, scales, k)
                if g == CHUNKS - 1:
                    closed.append((w, c))
            return closed

        r_of = {}
        rh_grouped_of = {}
        out_ps_of = {}

        def reset_sigmoid(c):
            r_of[c] = work.tile([P, PACK, B], F32, name="r_sb", tag="four_tiles")
            for t in range(PACK):
                i = c * PACK + t
                nc.scalar.activation(
                    out=r_of[c][:, t, :], in_=accs_of[(0, c)][t], func=ACT.Sigmoid, bias=bias_of[0][:, i : i + 1]
                )

        def reset_times_hidden(c):
            rh_grouped_of[c] = work.tile([P, B, PACK], BF16, name="rh_grouped", align_bytes=64)
            nc.vector.tensor_tensor(
                out=rh_grouped_of[c][:],
                in0=r_of[c][:].rearrange("p t b -> p b t"),
                in1=acts_grouped[:, c + 1, :, :],
                op=ALU.mult,
            )

        def reset_quantise(c):
            nc.vector.quantize_mx(
                out=rh_codes[:, c, :].bitcast(FP8X4),
                scales=rh_scales[:, c, :],
                in_=rh_grouped_of[c][:].rearrange("p b t -> p (b t)"),
            )

        def gate_silu(c):
            for t in range(PACK):
                i = c * PACK + t
                nc.scalar.activation(
                    out=silu_gate[:, i, :], in_=accs_of[(1, c)][t], func=ACT.Silu, bias=bias_of[1][:, i : i + 1]
                )

        product_of = {}

        def up_product(c):
            product = work.tile([P, PACK, B], F32, tag="four_tiles")
            product_of[c] = product
            for t in range(PACK):
                i = c * PACK + t
                nc.vector.scalar_tensor_tensor(
                    out=product[:, t, :],
                    in0=accs_of[(2, c)][t],
                    scalar=bias_of[2][:, i : i + 1],
                    in1=silu_gate[:, i, :],
                    op0=ALU.add,
                    op1=ALU.mult,
                )

        def up_transpose(c):
            product = product_of[c]
            for s in range(B_TILES):
                out_ps_of[(c, s)] = psum.tile([P, BLOCK], F32, name="out_ps", tag="bank%d" % (OUT_BANKS[c] + s))
                for t in range(PACK):
                    nc.tensor.transpose(
                        out_ps_of[(c, s)][:, t * P : (t + 1) * P], product[:, t, s * P : (s + 1) * P], ident_f32[:]
                    )

        def up_store(c, copies):
            for s in range(B_TILES):
                out_sb = stores.tile([P, BLOCK], F32)
                copies[s](out=out_sb[:], in_=out_ps_of[(c, s)][:])
                queue = nc.scalar if (c == BLOCKS - 1 and s == 0 and LAST_TWO_QUEUES) else nc.sync
                queue.dma_start(out=out[s * P : (s + 1) * P, c * BLOCK : (c + 1) * BLOCK], in_=out_sb[:])

        act_part = {}
        dve_part = {}
        store_part = {}
        waiting = []
        moving_ready = []
        owner = {}

        def banks_of(w, c):
            if shares_banks(w, c):
                return [pair_banks(w, c), pair_banks(w, c) + 1]
            return [PACK * (c % 2) + t for t in range(PACK)]

        def may_go(u):
            for step, j in units[u]:
                w, h, g = place_of(step)
                if (w == 0 or g == 0, g) not in moving_ready:
                    return False
                if g == 0 and any(bank in owner for bank in banks_of(w, 2 * h + j)):
                    return False
            return True

        def leave(w, c, banks):
            for bank in banks:
                if owner.get(bank) == (w, c):
                    owner.pop(bank)

        for it in range(STEPS + 12):
            act_now = act_part.get(it, [])
            dve_now = dve_part.get(it, [])
            if it < STEPS:
                grouped_of[it] = regroup.tile([P, HALF, PACK], BF16, name="grouped", align_bytes=64)
                share = SHARE_W_R if it < HALVES * CHUNKS else SHARE_NORMAL
                if any(w == 1 for w, c in act_now):
                    share = SHARE_SILU
                if it in route_units:
                    share = SHARE_ROUTE
                share = SHARES.get(it, share)
                regroup_cols(nc.vector.tensor_copy, it, 0, share)
                if it in route_units:
                    regroup_cols(nc.scalar.copy, it, share, BLOCK)
                    copy_passed(it)
                else:
                    regroup_cols(nc.scalar.copy, it, share, HALF)
            for w, c in dve_now:
                if w == 0:
                    reset_times_hidden(c)
            behind = 0 if (it < EARLY or it >= STEPS - LATE) else LQ
            while len(codes_of) < STEPS and len(codes_of) <= it - behind:
                waiting.append(len(codes_of))
                quantise(len(codes_of))
            for w, c in dve_now:
                if w == 0:
                    reset_quantise(c)
                    moving_ready.append((False, c + 1))
                else:
                    up_product(c)
                    leave(w, c, [bank for bank in banks_of(w, c) if bank not in (OUT_BANKS[c], OUT_BANKS[c] + 1)])
                    owner[OUT_BANKS[c]] = (w, c)
                    owner[OUT_BANKS[c] + 1] = (w, c)
            for w, c in act_now:
                if w == 0:
                    reset_sigmoid(c)
                else:
                    gate_silu(c)
                leave(w, c, banks_of(w, c))
            for w, c in store_part.get(it, []):
                if c != BLOCKS - 1:
                    up_store(c, [nc.scalar.copy, nc.scalar.copy])
                    leave(w, c, [OUT_BANKS[c], OUT_BANKS[c] + 1])
            for g in range(CHUNKS):
                if it == ACTS_BEHIND[g] + 1 + ACTS_Q_LAG:
                    quantise_acts(g)
                    moving_ready.append((True, g))
                if it == ACTS_BEHIND[g] + 1:
                    copy_acts(g)
            if it == BIAS_AT + 1:
                copy_biases()
            if it + 1 in route_units:
                pass_through(it + 1)
            queued = 0
            while len(waiting) > 0 and may_go(waiting[0]):
                u = waiting.pop(0)
                for step, j in units[u]:
                    w, h, g = place_of(step)
                    for bank in banks_of(w, 2 * h + j):
                        owner[bank] = (w, 2 * h + j)
                closed = passes(u)
                queued += 2 * PACK
                for w, c in closed:
                    at = it + (LAG_SECOND if shares_banks(w, c) else LAG_FIRST) + queued // PASSES_AN_ITERATION
                    if w == 0:
                        act_part.setdefault(at, []).append((w, c))
                        dve_part.setdefault(at + RH_LAG, []).append((w, c))
                    if w == 1:
                        act_part.setdefault(at, []).append((w, c))
                    if w == 2:
                        dve_part.setdefault(at, []).append((w, c))
                        store_part.setdefault(at + (0 if c == BLOCKS - 1 else STORE_LAG), []).append((w, c))
            for w, c in dve_now:
                if w == 2:
                    up_transpose(c)
                    if c == BLOCKS - 1:
                        up_store(c, [nc.scalar.copy, nc.vector.tensor_copy])
            for g in range(CHUNKS):
                if it == ACTS_BEHIND[g]:
                    transpose_acts(g)
            if it == BIAS_AT:
                transpose_biases()
            if it + RAW_BUFS < STEPS:
                load_next(it + RAW_BUFS)
